import numpy as np
import ml_dtypes


def mxq(x, axis, fmt="e4m3"):
    dtype, down = {"e4m3": (ml_dtypes.float8_e4m3fn, 7), "e5m2": (ml_dtypes.float8_e5m2, 14)}[fmt]
    v = np.moveaxis(np.asarray(x, np.float32).astype(ml_dtypes.bfloat16).astype(np.float64), axis, -1)
    blocks = v.reshape(v.shape[:-1] + (-1, 32))
    amax = np.abs(blocks).max(-1, keepdims=True)
    byte = np.maximum(np.where(amax > 0, np.frexp(amax)[1] - 1 + 127, 0) - down, 1)
    scale = np.exp2(byte - 127.0)
    codes = (blocks / scale).astype(np.float32).astype(dtype).astype(np.float64)
    return np.moveaxis((codes * scale).reshape(v.shape), -1, axis)


WIDE = False


def mx_kscale(k):
    if not WIDE:
        return np.ones(k)
    levels = np.array([10, -10, 5, -5, 0])
    if k % 512:
        return np.exp2(np.random.permutation(np.resize(levels, k // 32))).repeat(32)
    a = np.empty((k // 512, 16))
    for p in range(k // 512):
        a[p, :8] = np.random.permutation(np.resize(levels, 8))
        for g in range(8):
            far = levels[np.abs(levels - a[p, g]) >= 10]
            a[p, g + 8] = far[np.random.randint(len(far))]
    return np.exp2(a.ravel()).repeat(32)


BF16 = ml_dtypes.bfloat16


def bf(x):
    return np.asarray(x, np.float32).astype(BF16)


def f64(x):
    return np.asarray(x).astype(np.float64)


B, N, D, H, DH = 8, 512, 1024, 4, 128
EPS = 1e-5


def rotate_every_two(u):
    p = u.reshape(u.shape[:-1] + (-1, 2))
    return np.stack((-p[..., 1], p[..., 0]), axis=-1).reshape(u.shape)


def apply_rotary(u, sin, cos):
    return u * cos + rotate_every_two(u) * sin


def setup_inputs():
    s = mx_kscale(D)
    r = np.exp2(-np.random.uniform(0.0, 9.0, (B, N, 1)))
    inv_freq = 1.0 / 10000.0 ** (np.arange(0, DH, 2) / DH)
    freqs = np.repeat(np.arange(N)[:, None] * inv_freq[None, :], 2, axis=-1)
    return {"x": bf((np.random.standard_normal((B, N, D)) + 0.5) * r),
            "gamma": bf((1.0 + 0.1 * np.random.standard_normal(D)) * s),
            "wq": bf(np.random.standard_normal((D, H * DH)) * 2.0 / np.sqrt(D) / s[:, None]),
            "wk": bf(np.random.standard_normal((D, DH)) / np.sqrt(D) / s[:, None]),
            "wv": bf(np.random.standard_normal((D, DH)) / np.sqrt(D) / s[:, None]),
            "sin": bf(np.sin(freqs)), "cos": bf(np.cos(freqs))}


def reference(x, gamma, wq, wk, wv, sin, cos):
    x, sin, cos = f64(x), f64(sin), f64(cos)
    mean = x.mean(-1, keepdims=True)
    var = np.square(x).mean(-1, keepdims=True) - np.square(mean)
    xn = 1.0 / np.sqrt(var + EPS) * (x - mean) * f64(gamma)
    xq = mxq(xn, 2, "e4m3")
    q = xq @ mxq(f64(wq), 0, "e4m3")
    k = xq @ mxq(f64(wk), 0, "e4m3")
    v = xq @ mxq(f64(wv), 0, "e4m3")
    q = q.reshape(B, N, H, DH).transpose(0, 2, 1, 3) * DH ** -0.5
    return apply_rotary(q, sin, cos), apply_rotary(k, sin, cos), v

@@ -1,0 +1,321 @@
+from contextlib import ExitStack
+
+import concourse.mybir as mybir
+from concourse.masks import make_identity
+
+FP32 = mybir.dt.float32
+BF16 = mybir.dt.bfloat16
+U32 = mybir.dt.uint32
+U8 = mybir.dt.uint8
+FP8X4 = mybir.dt.float8_e4m3fn_x4
+ALU = mybir.AluOpType
+ACT = mybir.ActivationFunctionType
+
+B, N, D, H, DH = 8, 512, 1024, 4, 128
+EPS = 1e-5
+Q_SCALE = DH**-0.5
+
+P = 128
+PACK = 4
+PASSES = D // (P * PACK)
+TILES = N // P
+ROW_TILES = B * TILES
+HEADS = H + 1
+HALF = DH // 2
+Q_COLS = slice(0, H * DH)
+K_COLS = slice(H * DH, H * DH + DH)
+V_COLS = slice(H * DH + DH, H * DH + 2 * DH)
+KV_COLS = slice(H * DH, H * DH + 2 * DH)
+W_COLS = H * DH + 2 * DH
+
+SUM_LEAD = 8
+STAT_LEAD = 5
+Y_LEAD = 4
+T_LEAD = 3
+G_LEAD = 2
+MX_LEAD = 1
+VECTOR_SUM_ENTRIES = 1
+
+FLOPS = 2 * B * N * D * W_COLS
+
+
+def tile_attention_pa_t_kernel(tc, x, gamma, wq, wk, wv, sin, cos, out_0, out_1, out_2):
+    nc = tc.nc
+    with ExitStack() as ctx:
+        const = ctx.enter_context(tc.tile_pool(name="const", bufs=1))
+        x_pool = ctx.enter_context(tc.tile_pool(name="x_pool", bufs=B))
+        stat_pool = ctx.enter_context(tc.tile_pool(name="stat_pool", bufs=3))
+        unread_pool = ctx.enter_context(tc.tile_pool(name="unread_pool", bufs=4))
+        y_pool = ctx.enter_context(tc.tile_pool(name="y_pool", bufs=4))
+        mx_pool = ctx.enter_context(tc.tile_pool(name="mx_pool", bufs=3))
+        out_pool = ctx.enter_context(tc.tile_pool(name="out_pool", bufs=2))
+        xt_psum = ctx.enter_context(tc.psum_pool(name="xt_psum", bufs=2))
+        qkv_psum = ctx.enter_context(tc.psum_pool(name="qkv_psum", bufs=2))
+
+        ident = const.tile([P, P], FP32)
+        make_identity(nc, ident[:])
+
+        ctx.enter_context(tc.manual_schedule())
+
+        x_sb = [x_pool.tile([P, TILES, D], BF16, name="x_sb") for b in range(B)]
+
+        def load_x(b):
+            nc.sync.dma_start(out=x_sb[b][:], in_=x[b].rearrange("(p t) k -> p t k", t=TILES))
+
+        load_x(0)
+        load_x(1)
+        w_raw = const.tile([P, PASSES, PACK, W_COLS], BF16)
+        for g in range(PASSES):
+            k_rows = slice(g * P * PACK, (g + 1) * P * PACK)
+            nc.sync.dma_start(out=w_raw[:, g, :, Q_COLS], in_=wq[k_rows, :].rearrange("(p j) n -> p j n", j=PACK))
+        for g in range(PASSES):
+            k_rows = slice(g * P * PACK, (g + 1) * P * PACK)
+            nc.sync.dma_start(out=w_raw[:, g, :, K_COLS], in_=wk[k_rows, :].rearrange("(p j) n -> p j n", j=PACK))
+        for g in range(PASSES):
+            k_rows = slice(g * P * PACK, (g + 1) * P * PACK)
+            nc.sync.dma_start(out=w_raw[:, g, :, V_COLS], in_=wv[k_rows, :].rearrange("(p j) n -> p j n", j=PACK))
+        gamma_bf = const.tile([P, PASSES, PACK], BF16)
+        nc.sync.dma_start(out=gamma_bf[:], in_=gamma.rearrange("(g p j) -> p g j", g=PASSES, j=PACK))
+        cos_bf = const.tile([P, TILES, DH], BF16)
+        sin_bf = const.tile([P, TILES, DH], BF16)
+        nc.sync.dma_start(out=cos_bf[:], in_=cos.rearrange("(p t) d -> p t d", t=TILES))
+        nc.sync.dma_start(out=sin_bf[:], in_=sin.rearrange("(p t) d -> p t d", t=TILES))
+        for b in range(2, B):
+            load_x(b)
+
+        one = const.tile([P, 1], FP32)
+        nc.vector.memset(one[:], 1.0)
+        root_of_one = const.tile([P, 1], FP32)
+        nc.scalar.activation(out=root_of_one[:], in_=one[:], func=ACT.Sqrt)
+
+        cos_q = const.tile([P, TILES, DH], FP32)
+        nc.gpsimd.tensor_scalar(out=cos_q[:], in0=cos_bf[:], scalar1=Q_SCALE, scalar2=0.0, op0=ALU.mult, op1=ALU.add)
+        sin_q = const.tile([P, TILES, HALF, 2], FP32)
+        sin_k = const.tile([P, TILES, HALF, 2], FP32)
+        sin_pairs = sin_bf[:].rearrange("p t (i m) -> p t i m", m=2)
+        for table, factor in ((sin_q, Q_SCALE), (sin_k, 1.0)):
+            for member, sign in ((0, -1.0), (1, 1.0)):
+                nc.gpsimd.tensor_scalar(
+                    out=table[:, :, :, member],
+                    in0=sin_pairs[:, :, :, member],
+                    scalar1=sign * factor,
+                    scalar2=0.0,
+                    op0=ALU.mult,
+                    op1=ALU.add,
+                )
+
+        gamma_col = const.tile([P, PASSES, PACK], FP32)
+        w_codes = const.tile([P, PASSES, W_COLS], U32, align_bytes=64)
+        w_scales = const.tile([P, PASSES, W_COLS], U8, align_bytes=64)
+
+        def prepare_gamma_and_weights():
+            nc.vector.tensor_copy(out=gamma_col[:], in_=gamma_bf[:])
+            w_grouped = [
+                const.tile([P, W_COLS, PACK], BF16, name="w_grouped%d" % g, align_bytes=64) for g in range(PASSES)
+            ]
+            for g in range(PASSES):
+                nc.vector.tensor_copy(
+                    out=w_grouped[g][:], in_=w_raw[:, g, :, :].rearrange("p j n -> p n j")
+                )
+            for g in range(PASSES):
+                for cols in (Q_COLS, KV_COLS):
+                    nc.vector.quantize_mx(
+                        out=w_codes[:, g, cols].bitcast(FP8X4),
+                        scales=w_scales[:, g, cols],
+                        in_=w_grouped[g][:, cols, :].rearrange("p n j -> p (n j)"),
+                    )
+
+        sums = {}
+        squares = {}
+
+        def row_sums(i):
+            b, t = divmod(i, TILES)
+            if t == 0:
+                sums[b] = stat_pool.tile([P, TILES], FP32, name="sums")
+                squares[b] = stat_pool.tile([P, TILES], FP32, name="squares")
+                if b < VECTOR_SUM_ENTRIES:
+                    nc.vector.tensor_reduce(out=sums[b][:], in_=x_sb[b][:], axis=mybir.AxisListType.X, op=ALU.add)
+            scalar_work = [(ACT.Square, squares[b])] + ([(ACT.Identity, sums[b])] if b >= VECTOR_SUM_ENTRIES else [])
+            for func, total in scalar_work:
+                unread = unread_pool.tile([P, D], BF16, name="unread")
+                nc.scalar.activation(out=unread[:], in_=x_sb[b][:, t, :], func=func, accum_out=total[:, t : t + 1])
+
+        neg_mean = {}
+        std = {}
+        rstd = {}
+
+        def variance(b):
+            neg_mean[b] = stat_pool.tile([P, TILES], FP32, name="neg_mean")
+            nc.vector.tensor_scalar_mul(out=neg_mean[b][:], in0=sums[b][:], scalar1=-1.0 / D)
+            mean_sq = stat_pool.tile([P, TILES], FP32, name="mean_sq")
+            nc.vector.tensor_tensor(out=mean_sq[:], in0=neg_mean[b][:], in1=neg_mean[b][:], op=ALU.mult)
+            second = stat_pool.tile([P, TILES], FP32, name="second")
+            nc.vector.tensor_scalar(
+                out=second[:], in0=squares[b][:], scalar1=1.0 / D, scalar2=EPS, op0=ALU.mult, op1=ALU.add
+            )
+            var_eps = stat_pool.tile([P, TILES], FP32, name="var_eps")
+            nc.vector.tensor_tensor(out=var_eps[:], in0=second[:], in1=mean_sq[:], op=ALU.subtract)
+            std[b] = stat_pool.tile([P, TILES], FP32, name="std")
+            nc.scalar.activation(out=std[b][:], in_=var_eps[:], func=ACT.Sqrt)
+
+        shift = {}
+
+        def inverse_std(b):
+            rstd[b] = stat_pool.tile([P, TILES], FP32, name="rstd")
+            nc.vector.reciprocal(out=rstd[b][:], in_=std[b][:])
+            shift[b] = stat_pool.tile([P, TILES], FP32, name="shift")
+            nc.vector.tensor_tensor(out=shift[b][:], in0=neg_mean[b][:], in1=rstd[b][:], op=ALU.mult)
+
+        y = {}
+
+        def normalise(i):
+            b, t = divmod(i, TILES)
+            y[i] = y_pool.tile([P, PASSES, PACK, P], FP32, name="y")
+            x_rows = x_sb[b][:, t, :].rearrange("p (g m j) -> p g j m", g=PASSES, j=PACK)
+            row_rstd = rstd[b][:, t : t + 1]
+            row_shift = shift[b][:, t : t + 1]
+            if i % 2 == 0:
+                nc.gpsimd.tensor_scalar(
+                    out=y[i][:], in0=x_rows, scalar1=row_rstd, scalar2=row_shift, op0=ALU.mult, op1=ALU.add
+                )
+            else:
+                nc.scalar.activation(out=y[i][:], in_=x_rows, func=ACT.Identity, scale=row_rstd, bias=row_shift)
+
+        xt = {}
+        grouped = {}
+
+        def transpose(i):
+            xt[i] = [xt_psum.tile([P, PACK, P], FP32, name="xt") for g in range(PASSES)]
+            for g in range(PASSES):
+                for j in range(PACK):
+                    nc.tensor.transpose(xt[i][g][:, j, :], y[i][:, g, j, :], ident[:])
+
+        def scale_by_gamma(i):
+            grouped[i] = mx_pool.tile([P, PASSES, P, PACK], BF16, name="grouped", align_bytes=64)
+            for g in range(PASSES):
+                nc.vector.tensor_tensor(
+                    out=grouped[i][:, g, :, :],
+                    in0=xt[i][g][:].rearrange("p j r -> p r j"),
+                    in1=gamma_col[:, g, :].unsqueeze(1).to_broadcast([P, P, PACK]),
+                    op=ALU.mult,
+                )
+
+        codes = {}
+        scales = {}
+
+        def quantise(i):
+            codes[i] = mx_pool.tile([P, PASSES, P], U32, name="codes", align_bytes=64)
+            scales[i] = mx_pool.tile([P, PASSES, P], U8, name="scales", align_bytes=64)
+            nc.vector.quantize_mx(
+                out=codes[i][:].rearrange("p g r -> p (g r)").bitcast(FP8X4),
+                scales=scales[i][:].rearrange("p g r -> p (g r)"),
+                in_=grouped[i][:].rearrange("p g r j -> p (g r j)"),
+            )
+
+        q_ps = {}
+        k_ps = {}
+        v_ps = {}
+
+        def project(i):
+            b, t = divmod(i, TILES)
+            q_ps[i] = qkv_psum.tile([P, H * DH], FP32, name="q_ps")
+            if t == 0:
+                k_ps[b] = qkv_psum.tile([P, TILES, DH], FP32, name="k_ps")
+                v_ps[b] = qkv_psum.tile([P, TILES, DH], FP32, name="v_ps")
+            for acc, cols in ((q_ps[i][:], Q_COLS), (k_ps[b][:, t, :], K_COLS), (v_ps[b][:, t, :], V_COLS)):
+                for g in range(PASSES):
+                    nc.tensor.matmul_mx(
+                        out=acc,
+                        lhsT=codes[i][:, g, :].bitcast(FP8X4),
+                        lhsT_scale=scales[i][:, g, :],
+                        rhs=w_codes[:, g, cols].bitcast(FP8X4),
+                        rhs_scale=w_scales[:, g, cols],
+                        start=(g == 0),
+                        stop=(g == PASSES - 1),
+                    )
+
+        rotated = {}
+        sin_part = {}
+
+        def rotary_products(u, cos_table, sin_table, cos_out, sin_out):
+            nc.vector.tensor_tensor(out=cos_out, in0=u, in1=cos_table, op=ALU.mult)
+            swapped = u.rearrange("p a (i m) -> p a i m", m=2)[:, :, :, ::-1]
+            nc.vector.tensor_tensor(
+                out=sin_out.rearrange("p a (i m) -> p a i m", m=2), in0=swapped, in1=sin_table, op=ALU.mult
+            )
+
+        def rotary_sum(cos_out, sin_out):
+            nc.gpsimd.tensor_tensor(out=cos_out, in0=cos_out, in1=sin_out, op=ALU.add)
+
+        def rotate_q(i):
+            b, t = divmod(i, TILES)
+            if t == 0:
+                rotated[b] = out_pool.tile([P, HEADS, TILES, DH], FP32, name="rotated")
+                sin_part[b] = out_pool.tile([P, HEADS, TILES, DH], FP32, name="sin_part")
+            rotary_products(
+                u=q_ps[i][:].rearrange("p (h d) -> p h d", h=H),
+                cos_table=cos_q[:, t, :].unsqueeze(1).to_broadcast([P, H, DH]),
+                sin_table=sin_q[:, t, :, :].unsqueeze(1).to_broadcast([P, H, HALF, 2]),
+                cos_out=rotated[b][:, 0:H, t, :],
+                sin_out=sin_part[b][:, 0:H, t, :],
+            )
+
+        def sum_q(i):
+            b, t = divmod(i, TILES)
+            rotary_sum(rotated[b][:, 0:H, t, :], sin_part[b][:, 0:H, t, :])
+
+        v_sb = {}
+
+        def rotate_k_copy_v(b):
+            rotary_products(
+                u=k_ps[b][:],
+                cos_table=cos_bf[:],
+                sin_table=sin_k[:],
+                cos_out=rotated[b][:, H, :, :],
+                sin_out=sin_part[b][:, H, :, :],
+            )
+            v_sb[b] = out_pool.tile([P, TILES, DH], FP32, name="v_sb")
+            nc.scalar.copy(out=v_sb[b][:], in_=v_ps[b][:])
+
+        def sum_k_and_store(b):
+            rotary_sum(rotated[b][:, H, :, :], sin_part[b][:, H, :, :])
+            nc.sync.dma_start(out=out_0[b].rearrange("h (p t) d -> p h t d", t=TILES), in_=rotated[b][:, 0:H, :, :])
+            nc.sync.dma_start(out=out_1[b].rearrange("(p t) d -> p t d", t=TILES), in_=rotated[b][:, H, :, :])
+            nc.sync.dma_start(out=out_2[b].rearrange("(p t) d -> p t d", t=TILES), in_=v_sb[b][:])
+
+        def is_tile(i):
+            return 0 <= i < ROW_TILES
+
+        def starts_entry(i):
+            return is_tile(i) and i % TILES == 0
+
+        def ends_entry(i):
+            return is_tile(i) and i % TILES == TILES - 1
+
+        for s in range(-SUM_LEAD, ROW_TILES + 1):
+            if is_tile(s - 1):
+                sum_q(s - 1)
+            if ends_entry(s - 1):
+                sum_k_and_store((s - 1) // TILES)
+            if is_tile(s + SUM_LEAD):
+                row_sums(s + SUM_LEAD)
+            if is_tile(s + MX_LEAD):
+                project(s + MX_LEAD)
+            if is_tile(s + G_LEAD):
+                scale_by_gamma(s + G_LEAD)
+            if is_tile(s + T_LEAD):
+                transpose(s + T_LEAD)
+            if starts_entry(s + STAT_LEAD - 1):
+                inverse_std((s + STAT_LEAD - 1) // TILES)
+            if is_tile(s + Y_LEAD):
+                normalise(s + Y_LEAD)
+            if s + Y_LEAD == 0:
+                prepare_gamma_and_weights()
+            if is_tile(s):
+                rotate_q(s)
+            if ends_entry(s):
+                rotate_k_copy_v(s // TILES)
+            if is_tile(s + G_LEAD):
+                quantise(s + G_LEAD)
+            if starts_entry(s + STAT_LEAD):
+                variance((s + STAT_LEAD) // TILES)

@@ -86,7 +86,7 @@ def tile_attention_pa_t_kernel(tc, x, gamma, wq, wk, wv, sin, cos, out_0, out_1,
         one = const.tile([P, 1], FP32)
         nc.vector.memset(one[:], 1.0)
         root_of_one = const.tile([P, 1], FP32)
-        nc.scalar.activation(out=root_of_one[:], in_=one[:], func=ACT.Sqrt)
+        nc.scalar.activation(out=root_of_one[:], in_=one[:], func=ACT.Abs_reciprocal_sqrt)
 
         cos_q = const.tile([P, TILES, DH], FP32)
         nc.gpsimd.tensor_scalar(out=cos_q[:], in0=cos_bf[:], scalar1=Q_SCALE, scalar2=0.0, op0=ALU.mult, op1=ALU.add)
@@ -125,46 +125,45 @@ def tile_attention_pa_t_kernel(tc, x, gamma, wq, wk, wv, sin, cos, out_0, out_1,
                         in_=w_grouped[g][:, cols, :].rearrange("p n j -> p (n j)"),
                     )
 
-        sums = {}
-        squares = {}
+        neg_mean = {}
+        mean_sq = {}
 
         def row_sums(i):
             b, t = divmod(i, TILES)
             if t == 0:
-                sums[b] = stat_pool.tile([P, TILES], FP32, name="sums")
-                squares[b] = stat_pool.tile([P, TILES], FP32, name="squares")
+                neg_mean[b] = stat_pool.tile([P, TILES], FP32, name="neg_mean")
+                mean_sq[b] = stat_pool.tile([P, TILES], FP32, name="mean_sq")
                 if b < VECTOR_SUM_ENTRIES:
-                    nc.vector.tensor_reduce(out=sums[b][:], in_=x_sb[b][:], axis=mybir.AxisListType.X, op=ALU.add)
-            scalar_work = [(ACT.Square, squares[b])] + ([(ACT.Identity, sums[b])] if b >= VECTOR_SUM_ENTRIES else [])
-            for func, total in scalar_work:
+                    sums = stat_pool.tile([P, TILES], FP32, name="sums")
+                    nc.vector.tensor_reduce(out=sums[:], in_=x_sb[b][:], axis=mybir.AxisListType.X, op=ALU.add)
+                    nc.vector.tensor_scalar_mul(out=neg_mean[b][:], in0=sums[:], scalar1=-1.0 / D)
+            scalar_work = [(ACT.Square, D**-0.5, mean_sq[b])]
+            if b >= VECTOR_SUM_ENTRIES:
+                scalar_work.append((ACT.Identity, -1.0 / D, neg_mean[b]))
+            for func, factor, total in scalar_work:
                 unread = unread_pool.tile([P, D], BF16, name="unread")
-                nc.scalar.activation(out=unread[:], in_=x_sb[b][:, t, :], func=func, accum_out=total[:, t : t + 1])
+                nc.scalar.activation(
+                    out=unread[:], in_=x_sb[b][:, t, :], func=func, scale=factor, accum_out=total[:, t : t + 1]
+                )
 
-        neg_mean = {}
-        std = {}
         rstd = {}
-
-        def variance(b):
-            neg_mean[b] = stat_pool.tile([P, TILES], FP32, name="neg_mean")
-            nc.vector.tensor_scalar_mul(out=neg_mean[b][:], in0=sums[b][:], scalar1=-1.0 / D)
-            mean_sq = stat_pool.tile([P, TILES], FP32, name="mean_sq")
-            nc.vector.tensor_tensor(out=mean_sq[:], in0=neg_mean[b][:], in1=neg_mean[b][:], op=ALU.mult)
-            second = stat_pool.tile([P, TILES], FP32, name="second")
-            nc.vector.tensor_scalar(
-                out=second[:], in0=squares[b][:], scalar1=1.0 / D, scalar2=EPS, op0=ALU.mult, op1=ALU.add
-            )
-            var_eps = stat_pool.tile([P, TILES], FP32, name="var_eps")
-            nc.vector.tensor_tensor(out=var_eps[:], in0=second[:], in1=mean_sq[:], op=ALU.subtract)
-            std[b] = stat_pool.tile([P, TILES], FP32, name="std")
-            nc.scalar.activation(out=std[b][:], in_=var_eps[:], func=ACT.Sqrt)
-
         shift = {}
 
         def inverse_std(b):
+            minus = stat_pool.tile([P, TILES], FP32, name="minus")
             rstd[b] = stat_pool.tile([P, TILES], FP32, name="rstd")
-            nc.vector.reciprocal(out=rstd[b][:], in_=std[b][:])
             shift[b] = stat_pool.tile([P, TILES], FP32, name="shift")
-            nc.vector.tensor_tensor(out=shift[b][:], in0=neg_mean[b][:], in1=rstd[b][:], op=ALU.mult)
+            cols = [slice(t, t + 1) for t in range(TILES)]
+            for c in cols:
+                nc.scalar.activation(
+                    out=minus[:, c], in_=neg_mean[b][:, c], func=ACT.Identity, scale=neg_mean[b][:, c], bias=-EPS
+                )
+            for c in cols:
+                nc.scalar.activation(
+                    out=rstd[b][:, c], in_=mean_sq[b][:, c], func=ACT.Abs_reciprocal_sqrt, scale=-1.0, bias=minus[:, c]
+                )
+            for c in cols[1::2]:
+                nc.scalar.activation(out=shift[b][:, c], in_=rstd[b][:, c], func=ACT.Identity, scale=neg_mean[b][:, c])
 
         y = {}
 
@@ -173,13 +172,19 @@ def tile_attention_pa_t_kernel(tc, x, gamma, wq, wk, wv, sin, cos, out_0, out_1,
             y[i] = y_pool.tile([P, PASSES, PACK, P], FP32, name="y")
             x_rows = x_sb[b][:, t, :].rearrange("p (g m j) -> p g j m", g=PASSES, j=PACK)
             row_rstd = rstd[b][:, t : t + 1]
-            row_shift = shift[b][:, t : t + 1]
             if i % 2 == 0:
                 nc.gpsimd.tensor_scalar(
-                    out=y[i][:], in0=x_rows, scalar1=row_rstd, scalar2=row_shift, op0=ALU.mult, op1=ALU.add
+                    out=y[i][:],
+                    in0=x_rows,
+                    scalar1=neg_mean[b][:, t : t + 1],
+                    scalar2=row_rstd,
+                    op0=ALU.add,
+                    op1=ALU.mult,
                 )
             else:
-                nc.scalar.activation(out=y[i][:], in_=x_rows, func=ACT.Identity, scale=row_rstd, bias=row_shift)
+                nc.scalar.activation(
+                    out=y[i][:], in_=x_rows, func=ACT.Identity, scale=row_rstd, bias=shift[b][:, t : t + 1]
+                )
 
         xt = {}
         grouped = {}
@@ -305,8 +310,6 @@ def tile_attention_pa_t_kernel(tc, x, gamma, wq, wk, wv, sin, cos, out_0, out_1,
                 scale_by_gamma(s + G_LEAD)
             if is_tile(s + T_LEAD):
                 transpose(s + T_LEAD)
-            if starts_entry(s + STAT_LEAD - 1):
-                inverse_std((s + STAT_LEAD - 1) // TILES)
             if is_tile(s + Y_LEAD):
                 normalise(s + Y_LEAD)
             if s + Y_LEAD == 0:
@@ -318,4 +321,4 @@ def tile_attention_pa_t_kernel(tc, x, gamma, wq, wk, wv, sin, cos, out_0, out_1,
             if is_tile(s + G_LEAD):
                 quantise(s + G_LEAD)
             if starts_entry(s + STAT_LEAD):
-                variance((s + STAT_LEAD) // TILES)
+                inverse_std((s + STAT_LEAD) // TILES)

@@ -20,21 +20,25 @@ PACK = 4
 PASSES = D // (P * PACK)
 TILES = N // P
 ROW_TILES = B * TILES
+PAIR = 2
 HEADS = H + 1
 HALF = DH // 2
+BN_MAX = 512
 Q_COLS = slice(0, H * DH)
 K_COLS = slice(H * DH, H * DH + DH)
 V_COLS = slice(H * DH + DH, H * DH + 2 * DH)
 KV_COLS = slice(H * DH, H * DH + 2 * DH)
 W_COLS = H * DH + 2 * DH
 
-SUM_LEAD = 8
-STAT_LEAD = 5
-Y_LEAD = 4
-T_LEAD = 3
-G_LEAD = 2
+QUANT_TILES = 2
 MX_LEAD = 1
-VECTOR_SUM_ENTRIES = 1
+G_LEAD = QUANT_TILES
+T_LEAD = G_LEAD + 1
+Y_LEAD = G_LEAD + 2
+STAT_LEAD = G_LEAD + 3
+SUM_LEAD = G_LEAD + 4
+VECTOR_STAT_TILES = 2
+SCALAR_Y = 4
 
 FLOPS = 2 * B * N * D * W_COLS
 
@@ -44,13 +48,14 @@ def tile_attention_pa_t_kernel(tc, x, gamma, wq, wk, wv, sin, cos, out_0, out_1,
     with ExitStack() as ctx:
         const = ctx.enter_context(tc.tile_pool(name="const", bufs=1))
         x_pool = ctx.enter_context(tc.tile_pool(name="x_pool", bufs=B))
-        stat_pool = ctx.enter_context(tc.tile_pool(name="stat_pool", bufs=3))
-        unread_pool = ctx.enter_context(tc.tile_pool(name="unread_pool", bufs=4))
+        stat_pool = ctx.enter_context(tc.tile_pool(name="stat_pool", bufs=6))
+        unread_pool = ctx.enter_context(tc.tile_pool(name="unread_pool", bufs=2))
         y_pool = ctx.enter_context(tc.tile_pool(name="y_pool", bufs=4))
-        mx_pool = ctx.enter_context(tc.tile_pool(name="mx_pool", bufs=3))
+        mx_pool = ctx.enter_context(tc.tile_pool(name="mx_pool", bufs=2))
         out_pool = ctx.enter_context(tc.tile_pool(name="out_pool", bufs=2))
-        xt_psum = ctx.enter_context(tc.psum_pool(name="xt_psum", bufs=2))
-        qkv_psum = ctx.enter_context(tc.psum_pool(name="qkv_psum", bufs=2))
+        xt_psum = ctx.enter_context(tc.psum_pool(name="xt_psum", bufs=4))
+        q_psum = ctx.enter_context(tc.psum_pool(name="q_psum", bufs=2))
+        kv_psum = ctx.enter_context(tc.psum_pool(name="kv_psum", bufs=2))
 
         ident = const.tile([P, P], FP32)
         make_identity(nc, ident[:])
@@ -59,135 +64,141 @@ def tile_attention_pa_t_kernel(tc, x, gamma, wq, wk, wv, sin, cos, out_0, out_1,
 
         x_sb = [x_pool.tile([P, TILES, D], BF16, name="x_sb") for b in range(B)]
 
-        def load_x(b):
-            nc.sync.dma_start(out=x_sb[b][:], in_=x[b].rearrange("(p t) k -> p t k", t=TILES))
+        def load_x(b, tiles):
+            nc.sync.dma_start(out=x_sb[b][:, tiles, :], in_=x[b].rearrange("(p t) k -> p t k", t=TILES)[:, tiles, :])
 
-        load_x(0)
-        load_x(1)
-        w_raw = const.tile([P, PASSES, PACK, W_COLS], BF16)
-        for g in range(PASSES):
-            k_rows = slice(g * P * PACK, (g + 1) * P * PACK)
-            nc.sync.dma_start(out=w_raw[:, g, :, Q_COLS], in_=wq[k_rows, :].rearrange("(p j) n -> p j n", j=PACK))
-        for g in range(PASSES):
-            k_rows = slice(g * P * PACK, (g + 1) * P * PACK)
-            nc.sync.dma_start(out=w_raw[:, g, :, K_COLS], in_=wk[k_rows, :].rearrange("(p j) n -> p j n", j=PACK))
-        for g in range(PASSES):
-            k_rows = slice(g * P * PACK, (g + 1) * P * PACK)
-            nc.sync.dma_start(out=w_raw[:, g, :, V_COLS], in_=wv[k_rows, :].rearrange("(p j) n -> p j n", j=PACK))
+        wq_raw = const.tile([P, PASSES, PACK, H * DH], BF16)
+        wk_raw = const.tile([P, PASSES, PACK, DH], BF16)
+        wv_raw = const.tile([P, PASSES, PACK, DH], BF16)
         gamma_bf = const.tile([P, PASSES, PACK], BF16)
-        nc.sync.dma_start(out=gamma_bf[:], in_=gamma.rearrange("(g p j) -> p g j", g=PASSES, j=PACK))
         cos_bf = const.tile([P, TILES, DH], BF16)
         sin_bf = const.tile([P, TILES, DH], BF16)
+
+        load_x(0, slice(0, 1))
+        load_x(0, slice(1, 2))
+        nc.sync.dma_start(out=gamma_bf[:], in_=gamma.rearrange("(g p j) -> p g j", g=PASSES, j=PACK))
         nc.sync.dma_start(out=cos_bf[:], in_=cos.rearrange("(p t) d -> p t d", t=TILES))
         nc.sync.dma_start(out=sin_bf[:], in_=sin.rearrange("(p t) d -> p t d", t=TILES))
-        for b in range(2, B):
-            load_x(b)
+        load_x(0, slice(2, 3))
+        for g in range(PASSES):
+            k_rows = slice(g * P * PACK, (g + 1) * P * PACK)
+            nc.sync.dma_start(out=wq_raw[:, g, :, :], in_=wq[k_rows, :].rearrange("(p j) n -> p j n", j=PACK))
+        load_x(0, slice(3, 4))
+        nc.sync.dma_start(out=wk_raw[:], in_=wk.rearrange("(g p j) n -> p g j n", g=PASSES, j=PACK))
+        nc.sync.dma_start(out=wv_raw[:], in_=wv.rearrange("(g p j) n -> p g j n", g=PASSES, j=PACK))
+        for b in range(1, B):
+            load_x(b, slice(0, TILES))
 
         one = const.tile([P, 1], FP32)
         nc.vector.memset(one[:], 1.0)
         root_of_one = const.tile([P, 1], FP32)
         nc.scalar.activation(out=root_of_one[:], in_=one[:], func=ACT.Abs_reciprocal_sqrt)
 
+        sign = const.tile([P, HALF, 2], FP32)
+        nc.gpsimd.memset(sign[:, :, 0], -1.0)
+        nc.gpsimd.memset(sign[:, :, 1], 1.0)
         cos_q = const.tile([P, TILES, DH], FP32)
-        nc.gpsimd.tensor_scalar(out=cos_q[:], in0=cos_bf[:], scalar1=Q_SCALE, scalar2=0.0, op0=ALU.mult, op1=ALU.add)
-        sin_q = const.tile([P, TILES, HALF, 2], FP32)
-        sin_k = const.tile([P, TILES, HALF, 2], FP32)
-        sin_pairs = sin_bf[:].rearrange("p t (i m) -> p t i m", m=2)
-        for table, factor in ((sin_q, Q_SCALE), (sin_k, 1.0)):
-            for member, sign in ((0, -1.0), (1, 1.0)):
-                nc.gpsimd.tensor_scalar(
-                    out=table[:, :, :, member],
-                    in0=sin_pairs[:, :, :, member],
-                    scalar1=sign * factor,
-                    scalar2=0.0,
-                    op0=ALU.mult,
-                    op1=ALU.add,
-                )
-
+        sin_q = const.tile([P, TILES, DH], FP32)
+        sin_k = const.tile([P, TILES, DH], FP32)
         gamma_col = const.tile([P, PASSES, PACK], FP32)
+
+        def prepare_tables():
+            nc.gpsimd.tensor_copy(out=gamma_col[:], in_=gamma_bf[:])
+            nc.gpsimd.tensor_scalar(out=cos_q[:], in0=cos_bf[:], scalar1=Q_SCALE, scalar2=0.0, op0=ALU.mult, op1=ALU.add)
+            signs = sign[:].rearrange("p i m -> p (i m)").unsqueeze(1).to_broadcast([P, TILES, DH])
+            nc.gpsimd.tensor_tensor(out=sin_k[:], in0=sin_bf[:], in1=signs, op=ALU.mult)
+            nc.gpsimd.tensor_scalar(out=sin_q[:], in0=sin_k[:], scalar1=Q_SCALE, scalar2=0.0, op0=ALU.mult, op1=ALU.add)
+
+        w_grouped = [const.tile([P, W_COLS, PACK], BF16, name="w_grouped%d" % g, align_bytes=64) for g in range(PASSES)]
         w_codes = const.tile([P, PASSES, W_COLS], U32, align_bytes=64)
         w_scales = const.tile([P, PASSES, W_COLS], U8, align_bytes=64)
 
-        def prepare_gamma_and_weights():
-            nc.vector.tensor_copy(out=gamma_col[:], in_=gamma_bf[:])
-            w_grouped = [
-                const.tile([P, W_COLS, PACK], BF16, name="w_grouped%d" % g, align_bytes=64) for g in range(PASSES)
-            ]
-            for g in range(PASSES):
-                nc.vector.tensor_copy(
-                    out=w_grouped[g][:], in_=w_raw[:, g, :, :].rearrange("p j n -> p n j")
-                )
-            for g in range(PASSES):
-                for cols in (Q_COLS, KV_COLS):
-                    nc.vector.quantize_mx(
-                        out=w_codes[:, g, cols].bitcast(FP8X4),
-                        scales=w_scales[:, g, cols],
-                        in_=w_grouped[g][:, cols, :].rearrange("p n j -> p (n j)"),
-                    )
+        def group_weight(raw, g, cols):
+            nc.vector.tensor_copy(out=w_grouped[g][:, cols, :], in_=raw[:, g, :, :].rearrange("p j n -> p n j"))
+
+        def quantise_weights(g, cols):
+            nc.vector.quantize_mx(
+                out=w_codes[:, g, cols].bitcast(FP8X4),
+                scales=w_scales[:, g, cols],
+                in_=w_grouped[g][:, cols, :].rearrange("p n j -> p (n j)"),
+            )
 
         neg_mean = {}
-        mean_sq = {}
-
-        def row_sums(i):
-            b, t = divmod(i, TILES)
-            if t == 0:
-                neg_mean[b] = stat_pool.tile([P, TILES], FP32, name="neg_mean")
-                mean_sq[b] = stat_pool.tile([P, TILES], FP32, name="mean_sq")
-                if b < VECTOR_SUM_ENTRIES:
-                    sums = stat_pool.tile([P, TILES], FP32, name="sums")
-                    nc.vector.tensor_reduce(out=sums[:], in_=x_sb[b][:], axis=mybir.AxisListType.X, op=ALU.add)
-                    nc.vector.tensor_scalar_mul(out=neg_mean[b][:], in0=sums[:], scalar1=-1.0 / D)
-            scalar_work = [(ACT.Square, D**-0.5, mean_sq[b])]
-            if b >= VECTOR_SUM_ENTRIES:
-                scalar_work.append((ACT.Identity, -1.0 / D, neg_mean[b]))
-            for func, factor, total in scalar_work:
-                unread = unread_pool.tile([P, D], BF16, name="unread")
-                nc.scalar.activation(
-                    out=unread[:], in_=x_sb[b][:, t, :], func=func, scale=factor, accum_out=total[:, t : t + 1]
-                )
-
+        spread = {}
+        minus = {}
         rstd = {}
         shift = {}
-
-        def inverse_std(b):
-            minus = stat_pool.tile([P, TILES], FP32, name="minus")
-            rstd[b] = stat_pool.tile([P, TILES], FP32, name="rstd")
-            shift[b] = stat_pool.tile([P, TILES], FP32, name="shift")
-            cols = [slice(t, t + 1) for t in range(TILES)]
-            for c in cols:
-                nc.scalar.activation(
-                    out=minus[:, c], in_=neg_mean[b][:, c], func=ACT.Identity, scale=neg_mean[b][:, c], bias=-EPS
-                )
-            for c in cols:
-                nc.scalar.activation(
-                    out=rstd[b][:, c], in_=mean_sq[b][:, c], func=ACT.Abs_reciprocal_sqrt, scale=-1.0, bias=minus[:, c]
-                )
-            for c in cols[1::2]:
-                nc.scalar.activation(out=shift[b][:, c], in_=rstd[b][:, c], func=ACT.Identity, scale=neg_mean[b][:, c])
-
         y = {}
+        xt = {}
+        grouped = {}
+        codes = {}
+        scales = {}
+        q_ps = {}
+        kv_ps = {}
+        rotated = {}
+        sin_part = {}
+        v_sb = {}
+
+        def on_scalar(i):
+            return i % SCALAR_Y == 0
+
+        def vector_statistics(i):
+            b, t = divmod(i, TILES)
+            parts = stat_pool.tile([P, D // BN_MAX, 6], FP32, name="parts")
+            for h in range(D // BN_MAX):
+                nc.vector.bn_stats(out=parts[:, h, :], in_=x_sb[b][:, t, h * BN_MAX : (h + 1) * BN_MAX])
+            mean_var = stat_pool.tile([P, 2], FP32, name="mean_var")
+            nc.vector.bn_aggr(out=mean_var[:], in_=parts[:].rearrange("p h s -> p (h s)"))
+            neg_mean[i] = stat_pool.tile([P, 1], FP32, name="neg_mean")
+            nc.vector.tensor_scalar_mul(out=neg_mean[i][:], in0=mean_var[:, 0:1], scalar1=-1.0)
+            spread[i] = mean_var[:, 1:2]
+
+        def scalar_sum(i, func, factor, name):
+            b, t = divmod(i, TILES)
+            total = stat_pool.tile([P, 1], FP32, name=name)
+            unread = unread_pool.tile([P, D], BF16, name="unread")
+            nc.scalar.activation(out=unread[:], in_=x_sb[b][:, t, :], func=func, scale=factor, accum_out=total[:])
+            return total
+
+        def sum_squares(i):
+            if i < VECTOR_STAT_TILES:
+                vector_statistics(i)
+            else:
+                spread[i] = scalar_sum(i, ACT.Square, D**-0.5, "mean_sq")[:]
+
+        def sum_values(i):
+            if i >= VECTOR_STAT_TILES:
+                neg_mean[i] = scalar_sum(i, ACT.Identity, -1.0 / D, "neg_mean")
+
+        def mean_term(i):
+            if i >= VECTOR_STAT_TILES:
+                minus[i] = stat_pool.tile([P, 1], FP32, name="minus")
+                nc.scalar.activation(
+                    out=minus[i][:], in_=neg_mean[i][:], func=ACT.Identity, scale=neg_mean[i][:], bias=-EPS
+                )
+
+        def inverse_std(i):
+            rstd[i] = stat_pool.tile([P, 1], FP32, name="rstd")
+            if i < VECTOR_STAT_TILES:
+                nc.scalar.activation(out=rstd[i][:], in_=spread[i], func=ACT.Abs_reciprocal_sqrt, bias=EPS)
+            else:
+                nc.scalar.activation(
+                    out=rstd[i][:], in_=spread[i], func=ACT.Abs_reciprocal_sqrt, scale=-1.0, bias=minus[i][:]
+                )
+            if on_scalar(i):
+                shift[i] = stat_pool.tile([P, 1], FP32, name="shift")
+                nc.scalar.activation(out=shift[i][:], in_=rstd[i][:], func=ACT.Identity, scale=neg_mean[i][:])
 
         def normalise(i):
             b, t = divmod(i, TILES)
             y[i] = y_pool.tile([P, PASSES, PACK, P], FP32, name="y")
             x_rows = x_sb[b][:, t, :].rearrange("p (g m j) -> p g j m", g=PASSES, j=PACK)
-            row_rstd = rstd[b][:, t : t + 1]
-            if i % 2 == 0:
-                nc.gpsimd.tensor_scalar(
-                    out=y[i][:],
-                    in0=x_rows,
-                    scalar1=neg_mean[b][:, t : t + 1],
-                    scalar2=row_rstd,
-                    op0=ALU.add,
-                    op1=ALU.mult,
-                )
+            if on_scalar(i):
+                nc.scalar.activation(out=y[i][:], in_=x_rows, func=ACT.Identity, scale=rstd[i][:], bias=shift[i][:])
             else:
-                nc.scalar.activation(
-                    out=y[i][:], in_=x_rows, func=ACT.Identity, scale=row_rstd, bias=shift[b][:, t : t + 1]
+                nc.gpsimd.tensor_scalar(
+                    out=y[i][:], in0=x_rows, scalar1=neg_mean[i][:], scalar2=rstd[i][:], op0=ALU.add, op1=ALU.mult
                 )
-
-        xt = {}
-        grouped = {}
 
         def transpose(i):
             xt[i] = [xt_psum.tile([P, PACK, P], FP32, name="xt") for g in range(PASSES)]
@@ -196,129 +207,155 @@ def tile_attention_pa_t_kernel(tc, x, gamma, wq, wk, wv, sin, cos, out_0, out_1,
                     nc.tensor.transpose(xt[i][g][:, j, :], y[i][:, g, j, :], ident[:])
 
         def scale_by_gamma(i):
-            grouped[i] = mx_pool.tile([P, PASSES, P, PACK], BF16, name="grouped", align_bytes=64)
+            group, slot = divmod(i, QUANT_TILES)
+            if slot == 0:
+                grouped[group] = mx_pool.tile([P, QUANT_TILES, PASSES, P, PACK], BF16, name="grouped", align_bytes=64)
             for g in range(PASSES):
                 nc.vector.tensor_tensor(
-                    out=grouped[i][:, g, :, :],
+                    out=grouped[group][:, slot, g, :, :],
                     in0=xt[i][g][:].rearrange("p j r -> p r j"),
                     in1=gamma_col[:, g, :].unsqueeze(1).to_broadcast([P, P, PACK]),
                     op=ALU.mult,
                 )
 
-        codes = {}
-        scales = {}
-
-        def quantise(i):
-            codes[i] = mx_pool.tile([P, PASSES, P], U32, name="codes", align_bytes=64)
-            scales[i] = mx_pool.tile([P, PASSES, P], U8, name="scales", align_bytes=64)
+        def quantise(group):
+            codes[group] = mx_pool.tile([P, QUANT_TILES, PASSES, P], U32, name="codes", align_bytes=64)
+            scales[group] = mx_pool.tile([P, QUANT_TILES, PASSES, P], U8, name="scales", align_bytes=64)
             nc.vector.quantize_mx(
-                out=codes[i][:].rearrange("p g r -> p (g r)").bitcast(FP8X4),
-                scales=scales[i][:].rearrange("p g r -> p (g r)"),
-                in_=grouped[i][:].rearrange("p g r j -> p (g r j)"),
+                out=codes[group][:].rearrange("p s g r -> p (s g r)").bitcast(FP8X4),
+                scales=scales[group][:].rearrange("p s g r -> p (s g r)"),
+                in_=grouped[group][:].rearrange("p s g r j -> p (s g r j)"),
             )
 
-        q_ps = {}
-        k_ps = {}
-        v_ps = {}
-
         def project(i):
-            b, t = divmod(i, TILES)
-            q_ps[i] = qkv_psum.tile([P, H * DH], FP32, name="q_ps")
-            if t == 0:
-                k_ps[b] = qkv_psum.tile([P, TILES, DH], FP32, name="k_ps")
-                v_ps[b] = qkv_psum.tile([P, TILES, DH], FP32, name="v_ps")
-            for acc, cols in ((q_ps[i][:], Q_COLS), (k_ps[b][:, t, :], K_COLS), (v_ps[b][:, t, :], V_COLS)):
+            group, slot = divmod(i, QUANT_TILES)
+            pair, half = divmod(i, PAIR)
+            q_ps[i] = q_psum.tile([P, H * DH], FP32, name="q_ps")
+            if half == 0:
+                kv_ps[pair] = kv_psum.tile([P, PAIR, 2 * DH], FP32, name="kv_ps")
+            for acc, cols in ((q_ps[i][:], Q_COLS), (kv_ps[pair][:, half, :], KV_COLS)):
                 for g in range(PASSES):
                     nc.tensor.matmul_mx(
                         out=acc,
-                        lhsT=codes[i][:, g, :].bitcast(FP8X4),
-                        lhsT_scale=scales[i][:, g, :],
+                        lhsT=codes[group][:, slot, g, :].bitcast(FP8X4),
+                        lhsT_scale=scales[group][:, slot, g, :],
                         rhs=w_codes[:, g, cols].bitcast(FP8X4),
                         rhs_scale=w_scales[:, g, cols],
                         start=(g == 0),
                         stop=(g == PASSES - 1),
                     )
 
-        rotated = {}
-        sin_part = {}
-
         def rotary_products(u, cos_table, sin_table, cos_out, sin_out):
             nc.vector.tensor_tensor(out=cos_out, in0=u, in1=cos_table, op=ALU.mult)
             swapped = u.rearrange("p a (i m) -> p a i m", m=2)[:, :, :, ::-1]
             nc.vector.tensor_tensor(
-                out=sin_out.rearrange("p a (i m) -> p a i m", m=2), in0=swapped, in1=sin_table, op=ALU.mult
+                out=sin_out.rearrange("p a (i m) -> p a i m", m=2),
+                in0=swapped,
+                in1=sin_table.rearrange("p a (i m) -> p a i m", m=2),
+                op=ALU.mult,
             )
-
-        def rotary_sum(cos_out, sin_out):
-            nc.gpsimd.tensor_tensor(out=cos_out, in0=cos_out, in1=sin_out, op=ALU.add)
 
         def rotate_q(i):
             b, t = divmod(i, TILES)
             if t == 0:
                 rotated[b] = out_pool.tile([P, HEADS, TILES, DH], FP32, name="rotated")
                 sin_part[b] = out_pool.tile([P, HEADS, TILES, DH], FP32, name="sin_part")
+                v_sb[b] = out_pool.tile([P, TILES, DH], FP32, name="v_sb")
             rotary_products(
                 u=q_ps[i][:].rearrange("p (h d) -> p h d", h=H),
                 cos_table=cos_q[:, t, :].unsqueeze(1).to_broadcast([P, H, DH]),
-                sin_table=sin_q[:, t, :, :].unsqueeze(1).to_broadcast([P, H, HALF, 2]),
+                sin_table=sin_q[:, t, :].unsqueeze(1).to_broadcast([P, H, DH]),
                 cos_out=rotated[b][:, 0:H, t, :],
                 sin_out=sin_part[b][:, 0:H, t, :],
             )
 
+        def tiles_of_pair(pair):
+            b, t = divmod(pair * PAIR, TILES)
+            return b, slice(t, t + PAIR)
+
+        def rotate_k(pair):
+            b, ts = tiles_of_pair(pair)
+            rotary_products(
+                u=kv_ps[pair][:, :, 0:DH],
+                cos_table=cos_bf[:, ts, :],
+                sin_table=sin_k[:, ts, :],
+                cos_out=rotated[b][:, H, ts, :],
+                sin_out=sin_part[b][:, H, ts, :],
+            )
+
+        def copy_v(pair):
+            b, ts = tiles_of_pair(pair)
+            nc.scalar.copy(out=v_sb[b][:, ts, :], in_=kv_ps[pair][:, :, DH : 2 * DH])
+
+        def rotary_sum(engine, b, heads, ts):
+            engine.tensor_tensor(
+                out=rotated[b][:, heads, ts, :],
+                in0=rotated[b][:, heads, ts, :],
+                in1=sin_part[b][:, heads, ts, :],
+                op=ALU.add,
+            )
+
         def sum_q(i):
             b, t = divmod(i, TILES)
-            rotary_sum(rotated[b][:, 0:H, t, :], sin_part[b][:, 0:H, t, :])
+            rotary_sum(nc.gpsimd, b, slice(0, H), t)
 
-        v_sb = {}
+        def sum_k(pair):
+            b, ts = tiles_of_pair(pair)
+            rotary_sum(nc.gpsimd, b, H, ts)
 
-        def rotate_k_copy_v(b):
-            rotary_products(
-                u=k_ps[b][:],
-                cos_table=cos_bf[:],
-                sin_table=sin_k[:],
-                cos_out=rotated[b][:, H, :, :],
-                sin_out=sin_part[b][:, H, :, :],
+        def store(b, ts):
+            nc.sync.dma_start(
+                out=out_0[b].rearrange("h (p t) d -> p h t d", t=TILES)[:, :, ts, :], in_=rotated[b][:, 0:H, ts, :]
             )
-            v_sb[b] = out_pool.tile([P, TILES, DH], FP32, name="v_sb")
-            nc.scalar.copy(out=v_sb[b][:], in_=v_ps[b][:])
-
-        def sum_k_and_store(b):
-            rotary_sum(rotated[b][:, H, :, :], sin_part[b][:, H, :, :])
-            nc.sync.dma_start(out=out_0[b].rearrange("h (p t) d -> p h t d", t=TILES), in_=rotated[b][:, 0:H, :, :])
-            nc.sync.dma_start(out=out_1[b].rearrange("(p t) d -> p t d", t=TILES), in_=rotated[b][:, H, :, :])
-            nc.sync.dma_start(out=out_2[b].rearrange("(p t) d -> p t d", t=TILES), in_=v_sb[b][:])
+            nc.sync.dma_start(out=out_1[b].rearrange("(p t) d -> p t d", t=TILES)[:, ts, :], in_=rotated[b][:, H, ts, :])
+            nc.sync.dma_start(out=out_2[b].rearrange("(p t) d -> p t d", t=TILES)[:, ts, :], in_=v_sb[b][:, ts, :])
 
         def is_tile(i):
             return 0 <= i < ROW_TILES
 
-        def starts_entry(i):
-            return is_tile(i) and i % TILES == 0
-
-        def ends_entry(i):
-            return is_tile(i) and i % TILES == TILES - 1
+        def ends(i, size):
+            return is_tile(i) and i % size == size - 1
 
         for s in range(-SUM_LEAD, ROW_TILES + 1):
-            if is_tile(s - 1):
-                sum_q(s - 1)
-            if ends_entry(s - 1):
-                sum_k_and_store((s - 1) // TILES)
-            if is_tile(s + SUM_LEAD):
-                row_sums(s + SUM_LEAD)
-            if is_tile(s + MX_LEAD):
-                project(s + MX_LEAD)
-            if is_tile(s + G_LEAD):
-                scale_by_gamma(s + G_LEAD)
-            if is_tile(s + T_LEAD):
-                transpose(s + T_LEAD)
             if is_tile(s + Y_LEAD):
                 normalise(s + Y_LEAD)
-            if s + Y_LEAD == 0:
-                prepare_gamma_and_weights()
+            if is_tile(s + SUM_LEAD):
+                sum_squares(s + SUM_LEAD)
+            if is_tile(s + STAT_LEAD):
+                mean_term(s + STAT_LEAD)
+            if ends(s, PAIR):
+                copy_v(s // PAIR)
+            if is_tile(s + SUM_LEAD):
+                sum_values(s + SUM_LEAD)
+            if is_tile(s + STAT_LEAD):
+                inverse_std(s + STAT_LEAD)
+            if s + SUM_LEAD == 0:
+                prepare_tables()
+            if s + SUM_LEAD in (2, 3):
+                group_weight(wq_raw, s + SUM_LEAD - 2, Q_COLS)
+            if is_tile(s + G_LEAD):
+                scale_by_gamma(s + G_LEAD)
+            if s + G_LEAD == 0:
+                for g in range(PASSES):
+                    quantise_weights(g, Q_COLS)
+                for raw, cols in ((wk_raw, K_COLS), (wv_raw, V_COLS)):
+                    for g in range(PASSES):
+                        group_weight(raw, g, cols)
+                for g in range(PASSES):
+                    quantise_weights(g, KV_COLS)
+            if is_tile(s + T_LEAD):
+                transpose(s + T_LEAD)
+            if ends(s + G_LEAD, QUANT_TILES):
+                quantise((s + G_LEAD) // QUANT_TILES)
+            if is_tile(s + MX_LEAD):
+                project(s + MX_LEAD)
             if is_tile(s):
                 rotate_q(s)
-            if ends_entry(s):
-                rotate_k_copy_v(s // TILES)
-            if is_tile(s + G_LEAD):
-                quantise(s + G_LEAD)
-            if starts_entry(s + STAT_LEAD):
-                inverse_std((s + STAT_LEAD) // TILES)
+            if ends(s, PAIR):
+                rotate_k(s // PAIR)
+            if is_tile(s - 1):
+                sum_q(s - 1)
+            if ends(s - 1, PAIR):
+                sum_k((s - 1) // PAIR)
+            if ends(s - 1, TILES):
+                store((s - 1) // TILES, slice(0, TILES))

@@ -34,9 +34,9 @@ QUANT_TILES = 2
 MX_LEAD = 1
 G_LEAD = QUANT_TILES
 T_LEAD = G_LEAD + 1
-Y_LEAD = G_LEAD + 2
-STAT_LEAD = G_LEAD + 3
-SUM_LEAD = G_LEAD + 4
+Y_LEAD = G_LEAD + 3
+STAT_LEAD = G_LEAD + 4
+SUM_LEAD = G_LEAD + 5
 VECTOR_STAT_TILES = 2
 SCALAR_Y = 4
 
@@ -103,7 +103,6 @@ def tile_attention_pa_t_kernel(tc, x, gamma, wq, wk, wv, sin, cos, out_0, out_1,
         gamma_col = const.tile([P, PASSES, PACK], FP32)
 
         def prepare_tables():
-            nc.gpsimd.tensor_copy(out=gamma_col[:], in_=gamma_bf[:])
             nc.gpsimd.tensor_scalar(out=cos_q[:], in0=cos_bf[:], scalar1=Q_SCALE, scalar2=0.0, op0=ALU.mult, op1=ALU.add)
             signs = sign[:].rearrange("p i m -> p (i m)").unsqueeze(1).to_broadcast([P, TILES, DH])
             nc.gpsimd.tensor_tensor(out=sin_k[:], in0=sin_bf[:], in1=signs, op=ALU.mult)
@@ -297,18 +296,34 @@ def tile_attention_pa_t_kernel(tc, x, gamma, wq, wk, wv, sin, cos, out_0, out_1,
 
         def sum_q(i):
             b, t = divmod(i, TILES)
-            rotary_sum(nc.gpsimd, b, slice(0, H), t)
+            rotary_sum(nc.gpsimd, b, slice(0, H if i < ROW_TILES - 1 else H // 2), t)
 
         def sum_k(pair):
             b, ts = tiles_of_pair(pair)
-            rotary_sum(nc.gpsimd, b, H, ts)
+            if pair < ROW_TILES // PAIR - 1:
+                rotary_sum(nc.gpsimd, b, H, ts)
+            else:
+                rotary_sum(nc.vector, b, slice(H // 2, H), TILES - 1)
+                rotary_sum(nc.vector, b, H, ts)
 
-        def store(b, ts):
+        def store_q(b, ts):
             nc.sync.dma_start(
                 out=out_0[b].rearrange("h (p t) d -> p h t d", t=TILES)[:, :, ts, :], in_=rotated[b][:, 0:H, ts, :]
             )
+
+        def store_kv(b, ts):
             nc.sync.dma_start(out=out_1[b].rearrange("(p t) d -> p t d", t=TILES)[:, ts, :], in_=rotated[b][:, H, ts, :])
             nc.sync.dma_start(out=out_2[b].rearrange("(p t) d -> p t d", t=TILES)[:, ts, :], in_=v_sb[b][:, ts, :])
+
+        def store(i):
+            b, t = divmod(i, TILES)
+            if b == B - 1:
+                store_q(b, slice(t, t + 1))
+                if ends(i, PAIR):
+                    store_kv(*tiles_of_pair(i // PAIR))
+            elif ends(i, TILES):
+                store_q(b, slice(0, TILES))
+                store_kv(b, slice(0, TILES))
 
         def is_tile(i):
             return 0 <= i < ROW_TILES
@@ -317,22 +332,25 @@ def tile_attention_pa_t_kernel(tc, x, gamma, wq, wk, wv, sin, cos, out_0, out_1,
             return is_tile(i) and i % size == size - 1
 
         for s in range(-SUM_LEAD, ROW_TILES + 1):
-            if is_tile(s + Y_LEAD):
-                normalise(s + Y_LEAD)
-            if is_tile(s + SUM_LEAD):
-                sum_squares(s + SUM_LEAD)
-            if is_tile(s + STAT_LEAD):
-                mean_term(s + STAT_LEAD)
-            if ends(s, PAIR):
-                copy_v(s // PAIR)
-            if is_tile(s + SUM_LEAD):
-                sum_values(s + SUM_LEAD)
-            if is_tile(s + STAT_LEAD):
-                inverse_std(s + STAT_LEAD)
-            if s + SUM_LEAD == 0:
-                prepare_tables()
-            if s + SUM_LEAD in (2, 3):
-                group_weight(wq_raw, s + SUM_LEAD - 2, Q_COLS)
+            y_tile, stat_tile, sum_tile = s + Y_LEAD, s + STAT_LEAD, s + SUM_LEAD
+            if 0 <= stat_tile < VECTOR_STAT_TILES:
+                inverse_std(stat_tile)
+            if ends(s - 1, PAIR):
+                copy_v((s - 1) // PAIR)
+            if is_tile(y_tile) and on_scalar(y_tile):
+                normalise(y_tile)
+            if is_tile(sum_tile):
+                sum_squares(sum_tile)
+            if is_tile(stat_tile):
+                mean_term(stat_tile)
+            if is_tile(sum_tile):
+                sum_values(sum_tile)
+            if is_tile(stat_tile) and stat_tile >= VECTOR_STAT_TILES:
+                inverse_std(stat_tile)
+            if sum_tile == VECTOR_STAT_TILES:
+                nc.vector.tensor_copy(out=gamma_col[:], in_=gamma_bf[:])
+                for g in range(PASSES):
+                    group_weight(wq_raw, g, Q_COLS)
             if is_tile(s + G_LEAD):
                 scale_by_gamma(s + G_LEAD)
             if s + G_LEAD == 0:
@@ -345,17 +363,19 @@ def tile_attention_pa_t_kernel(tc, x, gamma, wq, wk, wv, sin, cos, out_0, out_1,
                     quantise_weights(g, KV_COLS)
             if is_tile(s + T_LEAD):
                 transpose(s + T_LEAD)
+            if is_tile(s):
+                rotate_q(s)
+                sum_q(s)
             if ends(s + G_LEAD, QUANT_TILES):
                 quantise((s + G_LEAD) // QUANT_TILES)
             if is_tile(s + MX_LEAD):
                 project(s + MX_LEAD)
-            if is_tile(s):
-                rotate_q(s)
             if ends(s, PAIR):
                 rotate_k(s // PAIR)
+                sum_k(s // PAIR)
+            if is_tile(y_tile) and not on_scalar(y_tile):
+                normalise(y_tile)
+            if y_tile == 1:
+                prepare_tables()
             if is_tile(s - 1):
-                sum_q(s - 1)
-            if ends(s - 1, PAIR):
-                sum_k((s - 1) // PAIR)
-            if ends(s - 1, TILES):
-                store((s - 1) // TILES, slice(0, TILES))
+                store(s - 1)

@@ -52,7 +52,7 @@ def tile_attention_pa_t_kernel(tc, x, gamma, wq, wk, wv, sin, cos, out_0, out_1,
         unread_pool = ctx.enter_context(tc.tile_pool(name="unread_pool", bufs=2))
         y_pool = ctx.enter_context(tc.tile_pool(name="y_pool", bufs=4))
         mx_pool = ctx.enter_context(tc.tile_pool(name="mx_pool", bufs=2))
-        out_pool = ctx.enter_context(tc.tile_pool(name="out_pool", bufs=2))
+        out_pool = ctx.enter_context(tc.tile_pool(name="out_pool", bufs=4))
         xt_psum = ctx.enter_context(tc.psum_pool(name="xt_psum", bufs=4))
         q_psum = ctx.enter_context(tc.psum_pool(name="q_psum", bufs=2))
         kv_psum = ctx.enter_context(tc.psum_pool(name="kv_psum", bufs=2))
@@ -255,17 +255,17 @@ def tile_attention_pa_t_kernel(tc, x, gamma, wq, wk, wv, sin, cos, out_0, out_1,
             )
 
         def rotate_q(i):
-            b, t = divmod(i, TILES)
-            if t == 0:
-                rotated[b] = out_pool.tile([P, HEADS, TILES, DH], FP32, name="rotated")
-                sin_part[b] = out_pool.tile([P, HEADS, TILES, DH], FP32, name="sin_part")
-                v_sb[b] = out_pool.tile([P, TILES, DH], FP32, name="v_sb")
+            pair, half = divmod(i, PAIR)
+            t = i % TILES
+            if half == 0:
+                rotated[pair] = out_pool.tile([P, HEADS, PAIR, DH], FP32, name="rotated")
+                sin_part[pair] = out_pool.tile([P, HEADS, PAIR, DH], FP32, name="sin_part")
             rotary_products(
                 u=q_ps[i][:].rearrange("p (h d) -> p h d", h=H),
                 cos_table=cos_q[:, t, :].unsqueeze(1).to_broadcast([P, H, DH]),
                 sin_table=sin_q[:, t, :].unsqueeze(1).to_broadcast([P, H, DH]),
-                cos_out=rotated[b][:, 0:H, t, :],
-                sin_out=sin_part[b][:, 0:H, t, :],
+                cos_out=rotated[pair][:, 0:H, half, :],
+                sin_out=sin_part[pair][:, 0:H, half, :],
             )
 
         def tiles_of_pair(pair):
@@ -278,52 +278,36 @@ def tile_attention_pa_t_kernel(tc, x, gamma, wq, wk, wv, sin, cos, out_0, out_1,
                 u=kv_ps[pair][:, :, 0:DH],
                 cos_table=cos_bf[:, ts, :],
                 sin_table=sin_k[:, ts, :],
-                cos_out=rotated[b][:, H, ts, :],
-                sin_out=sin_part[b][:, H, ts, :],
+                cos_out=rotated[pair][:, H, :, :],
+                sin_out=sin_part[pair][:, H, :, :],
             )
 
         def copy_v(pair):
-            b, ts = tiles_of_pair(pair)
-            nc.scalar.copy(out=v_sb[b][:, ts, :], in_=kv_ps[pair][:, :, DH : 2 * DH])
+            v_sb[pair] = out_pool.tile([P, PAIR, DH], FP32, name="v_sb")
+            nc.scalar.copy(out=v_sb[pair][:], in_=kv_ps[pair][:, :, DH : 2 * DH])
 
-        def rotary_sum(engine, b, heads, ts):
+        def rotary_sum(engine, pair, heads):
             engine.tensor_tensor(
-                out=rotated[b][:, heads, ts, :],
-                in0=rotated[b][:, heads, ts, :],
-                in1=sin_part[b][:, heads, ts, :],
+                out=rotated[pair][:, heads, :, :],
+                in0=rotated[pair][:, heads, :, :],
+                in1=sin_part[pair][:, heads, :, :],
                 op=ALU.add,
             )
 
-        def sum_q(i):
-            b, t = divmod(i, TILES)
-            rotary_sum(nc.gpsimd, b, slice(0, H if i < ROW_TILES - 1 else H // 2), t)
-
-        def sum_k(pair):
-            b, ts = tiles_of_pair(pair)
+        def sum_pair(pair):
             if pair < ROW_TILES // PAIR - 1:
-                rotary_sum(nc.gpsimd, b, H, ts)
+                rotary_sum(nc.gpsimd, pair, slice(0, HEADS))
             else:
-                rotary_sum(nc.vector, b, slice(H // 2, H), TILES - 1)
-                rotary_sum(nc.vector, b, H, ts)
+                rotary_sum(nc.gpsimd, pair, slice(0, H // 2))
+                rotary_sum(nc.vector, pair, slice(H // 2, HEADS))
 
-        def store_q(b, ts):
+        def store(pair):
+            b, ts = tiles_of_pair(pair)
             nc.sync.dma_start(
-                out=out_0[b].rearrange("h (p t) d -> p h t d", t=TILES)[:, :, ts, :], in_=rotated[b][:, 0:H, ts, :]
+                out=out_0[b].rearrange("h (p t) d -> p h t d", t=TILES)[:, :, ts, :], in_=rotated[pair][:, 0:H, :, :]
             )
-
-        def store_kv(b, ts):
-            nc.sync.dma_start(out=out_1[b].rearrange("(p t) d -> p t d", t=TILES)[:, ts, :], in_=rotated[b][:, H, ts, :])
-            nc.sync.dma_start(out=out_2[b].rearrange("(p t) d -> p t d", t=TILES)[:, ts, :], in_=v_sb[b][:, ts, :])
-
-        def store(i):
-            b, t = divmod(i, TILES)
-            if b == B - 1:
-                store_q(b, slice(t, t + 1))
-                if ends(i, PAIR):
-                    store_kv(*tiles_of_pair(i // PAIR))
-            elif ends(i, TILES):
-                store_q(b, slice(0, TILES))
-                store_kv(b, slice(0, TILES))
+            nc.sync.dma_start(out=out_1[b].rearrange("(p t) d -> p t d", t=TILES)[:, ts, :], in_=rotated[pair][:, H, :, :])
+            nc.sync.dma_start(out=out_2[b].rearrange("(p t) d -> p t d", t=TILES)[:, ts, :], in_=v_sb[pair][:])
 
         def is_tile(i):
             return 0 <= i < ROW_TILES
@@ -365,17 +349,16 @@ def tile_attention_pa_t_kernel(tc, x, gamma, wq, wk, wv, sin, cos, out_0, out_1,
                 transpose(s + T_LEAD)
             if is_tile(s):
                 rotate_q(s)
-                sum_q(s)
             if ends(s + G_LEAD, QUANT_TILES):
                 quantise((s + G_LEAD) // QUANT_TILES)
             if is_tile(s + MX_LEAD):
                 project(s + MX_LEAD)
             if ends(s, PAIR):
                 rotate_k(s // PAIR)
-                sum_k(s // PAIR)
+                sum_pair(s // PAIR)
             if is_tile(y_tile) and not on_scalar(y_tile):
                 normalise(y_tile)
             if y_tile == 1:
                 prepare_tables()
-            if is_tile(s - 1):
-                store(s - 1)
+            if ends(s - 1, PAIR):
+                store((s - 1) // PAIR)

@@ -24,21 +24,19 @@ PAIR = 2
 HEADS = H + 1
 HALF = DH // 2
 BN_MAX = 512
-Q_COLS = slice(0, H * DH)
-K_COLS = slice(H * DH, H * DH + DH)
-V_COLS = slice(H * DH + DH, H * DH + 2 * DH)
-KV_COLS = slice(H * DH, H * DH + 2 * DH)
 W_COLS = H * DH + 2 * DH
 
 QUANT_TILES = 2
 MX_LEAD = 1
 G_LEAD = QUANT_TILES
 T_LEAD = G_LEAD + 1
-Y_LEAD = G_LEAD + 3
-STAT_LEAD = G_LEAD + 4
-SUM_LEAD = G_LEAD + 5
+Y_LEAD = G_LEAD + 2
+STAT_LEAD = Y_LEAD + 1
+SUM_LEAD = Y_LEAD + 2
+FOLD_LEAD = SUM_LEAD + 1
 VECTOR_STAT_TILES = 2
-SCALAR_Y = 4
+FIRST_FOLD = TILES
+FOLDS = D // P
 
 FLOPS = 2 * B * N * D * W_COLS
 
@@ -53,12 +51,15 @@ def tile_attention_pa_t_kernel(tc, x, gamma, wq, wk, wv, sin, cos, out_0, out_1,
         y_pool = ctx.enter_context(tc.tile_pool(name="y_pool", bufs=4))
         mx_pool = ctx.enter_context(tc.tile_pool(name="mx_pool", bufs=2))
         out_pool = ctx.enter_context(tc.tile_pool(name="out_pool", bufs=4))
-        xt_psum = ctx.enter_context(tc.psum_pool(name="xt_psum", bufs=4))
+        xt_psum = ctx.enter_context(tc.psum_pool(name="xt_psum", bufs=3))
+        fold_psum = ctx.enter_context(tc.psum_pool(name="fold_psum", bufs=1))
         q_psum = ctx.enter_context(tc.psum_pool(name="q_psum", bufs=2))
         kv_psum = ctx.enter_context(tc.psum_pool(name="kv_psum", bufs=2))
 
         ident = const.tile([P, P], FP32)
         make_identity(nc, ident[:])
+        ident_bf = const.tile([P, P], BF16)
+        make_identity(nc, ident_bf[:])
 
         ctx.enter_context(tc.manual_schedule())
 
@@ -75,17 +76,17 @@ def tile_attention_pa_t_kernel(tc, x, gamma, wq, wk, wv, sin, cos, out_0, out_1,
         sin_bf = const.tile([P, TILES, DH], BF16)
 
         load_x(0, slice(0, 1))
+        nc.sync.dma_start(out=wk_raw[:], in_=wk.rearrange("(g p j) n -> p g j n", g=PASSES, j=PACK))
+        nc.sync.dma_start(out=wv_raw[:], in_=wv.rearrange("(g p j) n -> p g j n", g=PASSES, j=PACK))
         load_x(0, slice(1, 2))
         nc.sync.dma_start(out=gamma_bf[:], in_=gamma.rearrange("(g p j) -> p g j", g=PASSES, j=PACK))
-        nc.sync.dma_start(out=cos_bf[:], in_=cos.rearrange("(p t) d -> p t d", t=TILES))
-        nc.sync.dma_start(out=sin_bf[:], in_=sin.rearrange("(p t) d -> p t d", t=TILES))
-        load_x(0, slice(2, 3))
         for g in range(PASSES):
             k_rows = slice(g * P * PACK, (g + 1) * P * PACK)
             nc.sync.dma_start(out=wq_raw[:, g, :, :], in_=wq[k_rows, :].rearrange("(p j) n -> p j n", j=PACK))
+        load_x(0, slice(2, 3))
+        nc.sync.dma_start(out=cos_bf[:], in_=cos.rearrange("(p t) d -> p t d", t=TILES))
+        nc.sync.dma_start(out=sin_bf[:], in_=sin.rearrange("(p t) d -> p t d", t=TILES))
         load_x(0, slice(3, 4))
-        nc.sync.dma_start(out=wk_raw[:], in_=wk.rearrange("(g p j) n -> p g j n", g=PASSES, j=PACK))
-        nc.sync.dma_start(out=wv_raw[:], in_=wv.rearrange("(g p j) n -> p g j n", g=PASSES, j=PACK))
         for b in range(1, B):
             load_x(b, slice(0, TILES))
 
@@ -108,18 +109,34 @@ def tile_attention_pa_t_kernel(tc, x, gamma, wq, wk, wv, sin, cos, out_0, out_1,
             nc.gpsimd.tensor_tensor(out=sin_k[:], in0=sin_bf[:], in1=signs, op=ALU.mult)
             nc.gpsimd.tensor_scalar(out=sin_q[:], in0=sin_k[:], scalar1=Q_SCALE, scalar2=0.0, op0=ALU.mult, op1=ALU.add)
 
-        w_grouped = [const.tile([P, W_COLS, PACK], BF16, name="w_grouped%d" % g, align_bytes=64) for g in range(PASSES)]
-        w_codes = const.tile([P, PASSES, W_COLS], U32, align_bytes=64)
-        w_scales = const.tile([P, PASSES, W_COLS], U8, align_bytes=64)
+        w_grouped = {}
+        w_codes = {}
+        w_scales = {}
+        for part, width in (("q", H * DH), ("kv", 2 * DH)):
+            w_grouped[part] = const.tile([P, PASSES, width, PACK], BF16, name="w_grouped_" + part, align_bytes=64)
+            w_codes[part] = const.tile([P, PASSES, width], U32, name="w_codes_" + part, align_bytes=64)
+            w_scales[part] = const.tile([P, PASSES, width], U8, name="w_scales_" + part, align_bytes=64)
 
-        def group_weight(raw, g, cols):
-            nc.vector.tensor_copy(out=w_grouped[g][:, cols, :], in_=raw[:, g, :, :].rearrange("p j n -> p n j"))
+        def group_wq(g):
+            nc.vector.tensor_copy(out=w_grouped["q"][:, g, :, :], in_=wq_raw[:, g, :, :].rearrange("p j n -> p n j"))
 
-        def quantise_weights(g, cols):
+        def group_wk_wv():
+            for raw, cols in ((wk_raw, slice(0, DH)), (wv_raw, slice(DH, 2 * DH))):
+                for g in range(PASSES):
+                    nc.gpsimd.tensor_scalar(
+                        out=w_grouped["kv"][:, g, cols, :],
+                        in0=raw[:, g, :, :].rearrange("p j n -> p n j"),
+                        scalar1=1.0,
+                        scalar2=0.0,
+                        op0=ALU.mult,
+                        op1=ALU.add,
+                    )
+
+        def quantise_weights(part):
             nc.vector.quantize_mx(
-                out=w_codes[:, g, cols].bitcast(FP8X4),
-                scales=w_scales[:, g, cols],
-                in_=w_grouped[g][:, cols, :].rearrange("p n j -> p (n j)"),
+                out=w_codes[part][:].rearrange("p g n -> p (g n)").bitcast(FP8X4),
+                scales=w_scales[part][:].rearrange("p g n -> p (g n)"),
+                in_=w_grouped[part][:].rearrange("p g n j -> p (g n j)"),
             )
 
         neg_mean = {}
@@ -139,7 +156,7 @@ def tile_attention_pa_t_kernel(tc, x, gamma, wq, wk, wv, sin, cos, out_0, out_1,
         v_sb = {}
 
         def on_scalar(i):
-            return i % SCALAR_Y == 0
+            return i == 0 or i % 2 == 1
 
         def vector_statistics(i):
             b, t = divmod(i, TILES)
@@ -152,22 +169,43 @@ def tile_attention_pa_t_kernel(tc, x, gamma, wq, wk, wv, sin, cos, out_0, out_1,
             nc.vector.tensor_scalar_mul(out=neg_mean[i][:], in0=mean_var[:, 0:1], scalar1=-1.0)
             spread[i] = mean_var[:, 1:2]
 
-        def scalar_sum(i, func, factor, name):
-            b, t = divmod(i, TILES)
+        def scalar_sum(values, func, factor, name):
             total = stat_pool.tile([P, 1], FP32, name=name)
             unread = unread_pool.tile([P, D], BF16, name="unread")
-            nc.scalar.activation(out=unread[:], in_=x_sb[b][:, t, :], func=func, scale=factor, accum_out=total[:])
+            nc.scalar.activation(
+                out=unread[:, 0 : values.shape[-1]], in_=values, func=func, scale=factor, accum_out=total[:]
+            )
             return total
+
+        def folded(i):
+            return i >= FIRST_FOLD and i % 3 != 1
+
+        fold_ps = {}
+
+        def fold(i):
+            b, t = divmod(i, TILES)
+            fold_ps[i] = fold_psum.tile([P, P], FP32, name="fold_ps")
+            for c in range(FOLDS):
+                nc.tensor.matmul(
+                    fold_ps[i][:],
+                    lhsT=ident_bf[:],
+                    rhs=x_sb[b][:, t, c * P : (c + 1) * P],
+                    start=(c == 0),
+                    stop=(c == FOLDS - 1),
+                )
 
         def sum_squares(i):
             if i < VECTOR_STAT_TILES:
                 vector_statistics(i)
             else:
-                spread[i] = scalar_sum(i, ACT.Square, D**-0.5, "mean_sq")[:]
+                b, t = divmod(i, TILES)
+                spread[i] = scalar_sum(x_sb[b][:, t, :], ACT.Square, D**-0.5, "mean_sq")[:]
 
         def sum_values(i):
             if i >= VECTOR_STAT_TILES:
-                neg_mean[i] = scalar_sum(i, ACT.Identity, -1.0 / D, "neg_mean")
+                b, t = divmod(i, TILES)
+                values = fold_ps[i][:] if folded(i) else x_sb[b][:, t, :]
+                neg_mean[i] = scalar_sum(values, ACT.Identity, -1.0 / D, "neg_mean")
 
         def mean_term(i):
             if i >= VECTOR_STAT_TILES:
@@ -184,6 +222,8 @@ def tile_attention_pa_t_kernel(tc, x, gamma, wq, wk, wv, sin, cos, out_0, out_1,
                 nc.scalar.activation(
                     out=rstd[i][:], in_=spread[i], func=ACT.Abs_reciprocal_sqrt, scale=-1.0, bias=minus[i][:]
                 )
+
+        def shift_by_mean(i):
             if on_scalar(i):
                 shift[i] = stat_pool.tile([P, 1], FP32, name="shift")
                 nc.scalar.activation(out=shift[i][:], in_=rstd[i][:], func=ACT.Identity, scale=neg_mean[i][:])
@@ -232,14 +272,14 @@ def tile_attention_pa_t_kernel(tc, x, gamma, wq, wk, wv, sin, cos, out_0, out_1,
             q_ps[i] = q_psum.tile([P, H * DH], FP32, name="q_ps")
             if half == 0:
                 kv_ps[pair] = kv_psum.tile([P, PAIR, 2 * DH], FP32, name="kv_ps")
-            for acc, cols in ((q_ps[i][:], Q_COLS), (kv_ps[pair][:, half, :], KV_COLS)):
+            for acc, part in ((q_ps[i][:], "q"), (kv_ps[pair][:, half, :], "kv")):
                 for g in range(PASSES):
                     nc.tensor.matmul_mx(
                         out=acc,
                         lhsT=codes[group][:, slot, g, :].bitcast(FP8X4),
                         lhsT_scale=scales[group][:, slot, g, :],
-                        rhs=w_codes[:, g, cols].bitcast(FP8X4),
-                        rhs_scale=w_scales[:, g, cols],
+                        rhs=w_codes[part][:, g, :].bitcast(FP8X4),
+                        rhs_scale=w_scales[part][:, g, :],
                         start=(g == 0),
                         stop=(g == PASSES - 1),
                     )
@@ -272,6 +312,10 @@ def tile_attention_pa_t_kernel(tc, x, gamma, wq, wk, wv, sin, cos, out_0, out_1,
             b, t = divmod(pair * PAIR, TILES)
             return b, slice(t, t + PAIR)
 
+        def copy_v(pair):
+            v_sb[pair] = out_pool.tile([P, PAIR, DH], FP32, name="v_sb")
+            nc.scalar.copy(out=v_sb[pair][:], in_=kv_ps[pair][:, :, DH : 2 * DH])
+
         def rotate_k(pair):
             b, ts = tiles_of_pair(pair)
             rotary_products(
@@ -282,24 +326,20 @@ def tile_attention_pa_t_kernel(tc, x, gamma, wq, wk, wv, sin, cos, out_0, out_1,
                 sin_out=sin_part[pair][:, H, :, :],
             )
 
-        def copy_v(pair):
-            v_sb[pair] = out_pool.tile([P, PAIR, DH], FP32, name="v_sb")
-            nc.scalar.copy(out=v_sb[pair][:], in_=kv_ps[pair][:, :, DH : 2 * DH])
-
-        def rotary_sum(engine, pair, heads):
+        def rotary_sum(engine, pair, heads, halves):
             engine.tensor_tensor(
-                out=rotated[pair][:, heads, :, :],
-                in0=rotated[pair][:, heads, :, :],
-                in1=sin_part[pair][:, heads, :, :],
+                out=rotated[pair][:, heads, halves, :],
+                in0=rotated[pair][:, heads, halves, :],
+                in1=sin_part[pair][:, heads, halves, :],
                 op=ALU.add,
             )
 
-        def sum_pair(pair):
-            if pair < ROW_TILES // PAIR - 1:
-                rotary_sum(nc.gpsimd, pair, slice(0, HEADS))
-            else:
-                rotary_sum(nc.gpsimd, pair, slice(0, H // 2))
-                rotary_sum(nc.vector, pair, slice(H // 2, HEADS))
+        def sum_q(i):
+            pair, half = divmod(i, PAIR)
+            rotary_sum(nc.gpsimd if i < ROW_TILES - 1 else nc.vector, pair, slice(0, H), half)
+
+        def sum_k(pair):
+            rotary_sum(nc.gpsimd, pair, H, slice(0, PAIR))
 
         def store(pair):
             b, ts = tiles_of_pair(pair)
@@ -316,49 +356,57 @@ def tile_attention_pa_t_kernel(tc, x, gamma, wq, wk, wv, sin, cos, out_0, out_1,
             return is_tile(i) and i % size == size - 1
 
         for s in range(-SUM_LEAD, ROW_TILES + 1):
-            y_tile, stat_tile, sum_tile = s + Y_LEAD, s + STAT_LEAD, s + SUM_LEAD
+            y_tile, stat_tile, sum_tile, fold_tile = s + Y_LEAD, s + STAT_LEAD, s + SUM_LEAD, s + FOLD_LEAD
+            if sum_tile == 0:
+                group_wk_wv()
             if 0 <= stat_tile < VECTOR_STAT_TILES:
                 inverse_std(stat_tile)
+                shift_by_mean(stat_tile)
+            if is_tile(y_tile) and not on_scalar(y_tile):
+                normalise(y_tile)
+            if sum_tile == VECTOR_STAT_TILES + 1:
+                prepare_tables()
+            if is_tile(stat_tile):
+                mean_term(stat_tile)
             if ends(s - 1, PAIR):
                 copy_v((s - 1) // PAIR)
-            if is_tile(y_tile) and on_scalar(y_tile):
+            if y_tile == 0:
                 normalise(y_tile)
             if is_tile(sum_tile):
                 sum_squares(sum_tile)
-            if is_tile(stat_tile):
-                mean_term(stat_tile)
-            if is_tile(sum_tile):
-                sum_values(sum_tile)
             if is_tile(stat_tile) and stat_tile >= VECTOR_STAT_TILES:
                 inverse_std(stat_tile)
+            if is_tile(sum_tile):
+                sum_values(sum_tile)
+            if is_tile(y_tile) and on_scalar(y_tile) and y_tile > 0:
+                normalise(y_tile)
+            if is_tile(stat_tile) and stat_tile >= VECTOR_STAT_TILES:
+                shift_by_mean(stat_tile)
             if sum_tile == VECTOR_STAT_TILES:
                 nc.vector.tensor_copy(out=gamma_col[:], in_=gamma_bf[:])
-                for g in range(PASSES):
-                    group_weight(wq_raw, g, Q_COLS)
+                group_wq(0)
             if is_tile(s + G_LEAD):
                 scale_by_gamma(s + G_LEAD)
             if s + G_LEAD == 0:
-                for g in range(PASSES):
-                    quantise_weights(g, Q_COLS)
-                for raw, cols in ((wk_raw, K_COLS), (wv_raw, V_COLS)):
-                    for g in range(PASSES):
-                        group_weight(raw, g, cols)
-                for g in range(PASSES):
-                    quantise_weights(g, KV_COLS)
+                group_wq(1)
+                quantise_weights("q")
+                quantise_weights("kv")
             if is_tile(s + T_LEAD):
                 transpose(s + T_LEAD)
+            if s == ROW_TILES - 1:
+                rotate_k(s // PAIR)
+                sum_k(s // PAIR)
             if is_tile(s):
                 rotate_q(s)
+                sum_q(s)
             if ends(s + G_LEAD, QUANT_TILES):
                 quantise((s + G_LEAD) // QUANT_TILES)
             if is_tile(s + MX_LEAD):
                 project(s + MX_LEAD)
-            if ends(s, PAIR):
+            if is_tile(fold_tile) and folded(fold_tile):
+                fold(fold_tile)
+            if ends(s, PAIR) and s < ROW_TILES - 1:
                 rotate_k(s // PAIR)
-                sum_pair(s // PAIR)
-            if is_tile(y_tile) and not on_scalar(y_tile):
-                normalise(y_tile)
-            if y_tile == 1:
-                prepare_tables()
+                sum_k(s // PAIR)
             if ends(s - 1, PAIR):
                 store((s - 1) // PAIR)

@@ -120,17 +120,16 @@ def tile_attention_pa_t_kernel(tc, x, gamma, wq, wk, wv, sin, cos, out_0, out_1,
         def group_wq(g):
             nc.vector.tensor_copy(out=w_grouped["q"][:, g, :, :], in_=wq_raw[:, g, :, :].rearrange("p j n -> p n j"))
 
-        def group_wk_wv():
-            for raw, cols in ((wk_raw, slice(0, DH)), (wv_raw, slice(DH, 2 * DH))):
-                for g in range(PASSES):
-                    nc.gpsimd.tensor_scalar(
-                        out=w_grouped["kv"][:, g, cols, :],
-                        in0=raw[:, g, :, :].rearrange("p j n -> p n j"),
-                        scalar1=1.0,
-                        scalar2=0.0,
-                        op0=ALU.mult,
-                        op1=ALU.add,
-                    )
+        def group_wk_or_wv(raw, cols):
+            for g in range(PASSES):
+                nc.gpsimd.tensor_scalar(
+                    out=w_grouped["kv"][:, g, cols, :],
+                    in0=raw[:, g, :, :].rearrange("p j n -> p n j"),
+                    scalar1=1.0,
+                    scalar2=0.0,
+                    op0=ALU.mult,
+                    op1=ALU.add,
+                )
 
         def quantise_weights(part):
             nc.vector.quantize_mx(
@@ -156,7 +155,7 @@ def tile_attention_pa_t_kernel(tc, x, gamma, wq, wk, wv, sin, cos, out_0, out_1,
         v_sb = {}
 
         def on_scalar(i):
-            return i == 0 or i % 2 == 1
+            return i < TILES or i % 2 == 1
 
         def vector_statistics(i):
             b, t = divmod(i, TILES)
@@ -357,38 +356,38 @@ def tile_attention_pa_t_kernel(tc, x, gamma, wq, wk, wv, sin, cos, out_0, out_1,
 
         for s in range(-SUM_LEAD, ROW_TILES + 1):
             y_tile, stat_tile, sum_tile, fold_tile = s + Y_LEAD, s + STAT_LEAD, s + SUM_LEAD, s + FOLD_LEAD
-            if sum_tile == 0:
-                group_wk_wv()
+            if sum_tile == 1:
+                group_wk_or_wv(wk_raw, slice(0, DH))
+            if sum_tile == 3:
+                prepare_tables()
+                group_wk_or_wv(wv_raw, slice(DH, 2 * DH))
             if 0 <= stat_tile < VECTOR_STAT_TILES:
                 inverse_std(stat_tile)
                 shift_by_mean(stat_tile)
+                normalise(stat_tile)
             if is_tile(y_tile) and not on_scalar(y_tile):
                 normalise(y_tile)
-            if sum_tile == VECTOR_STAT_TILES + 1:
-                prepare_tables()
             if is_tile(stat_tile):
                 mean_term(stat_tile)
             if ends(s - 1, PAIR):
                 copy_v((s - 1) // PAIR)
-            if y_tile == 0:
-                normalise(y_tile)
             if is_tile(sum_tile):
                 sum_squares(sum_tile)
             if is_tile(stat_tile) and stat_tile >= VECTOR_STAT_TILES:
                 inverse_std(stat_tile)
             if is_tile(sum_tile):
                 sum_values(sum_tile)
-            if is_tile(y_tile) and on_scalar(y_tile) and y_tile > 0:
+            if is_tile(y_tile) and on_scalar(y_tile) and y_tile >= VECTOR_STAT_TILES:
                 normalise(y_tile)
             if is_tile(stat_tile) and stat_tile >= VECTOR_STAT_TILES:
                 shift_by_mean(stat_tile)
             if sum_tile == VECTOR_STAT_TILES:
                 nc.vector.tensor_copy(out=gamma_col[:], in_=gamma_bf[:])
                 group_wq(0)
+                group_wq(1)
             if is_tile(s + G_LEAD):
                 scale_by_gamma(s + G_LEAD)
-            if s + G_LEAD == 0:
-                group_wq(1)
+            if s + G_LEAD == 1:
                 quantise_weights("q")
                 quantise_weights("kv")
             if is_tile(s + T_LEAD):

@@ -35,7 +35,7 @@ STAT_LEAD = Y_LEAD + 1
 SUM_LEAD = Y_LEAD + 2
 FOLD_LEAD = SUM_LEAD + 1
 VECTOR_STAT_TILES = 2
-FIRST_FOLD = TILES
+LAST_FOLDED = ROW_TILES - 3
 FOLDS = D // P
 
 FLOPS = 2 * B * N * D * W_COLS
@@ -177,7 +177,7 @@ def tile_attention_pa_t_kernel(tc, x, gamma, wq, wk, wv, sin, cos, out_0, out_1,
             return total
 
         def folded(i):
-            return i >= FIRST_FOLD and i % 3 != 1
+            return VECTOR_STAT_TILES <= i <= LAST_FOLDED and i % 3 != 1
 
         fold_ps = {}
 
@@ -365,6 +365,8 @@ def tile_attention_pa_t_kernel(tc, x, gamma, wq, wk, wv, sin, cos, out_0, out_1,
                 inverse_std(stat_tile)
                 shift_by_mean(stat_tile)
                 normalise(stat_tile)
+            if stat_tile == 0:
+                transpose(stat_tile)
             if is_tile(y_tile) and not on_scalar(y_tile):
                 normalise(y_tile)
             if is_tile(stat_tile):
@@ -390,7 +392,7 @@ def tile_attention_pa_t_kernel(tc, x, gamma, wq, wk, wv, sin, cos, out_0, out_1,
             if s + G_LEAD == 1:
                 quantise_weights("q")
                 quantise_weights("kv")
-            if is_tile(s + T_LEAD):
+            if is_tile(s + T_LEAD) and s + T_LEAD > 0:
                 transpose(s + T_LEAD)
             if s == ROW_TILES - 1:
                 rotate_k(s // PAIR)

from contextlib import ExitStack

import concourse.mybir as mybir
from concourse.masks import make_identity

FP32 = mybir.dt.float32
BF16 = mybir.dt.bfloat16
U32 = mybir.dt.uint32
U8 = mybir.dt.uint8
FP8X4 = mybir.dt.float8_e4m3fn_x4
ALU = mybir.AluOpType
ACT = mybir.ActivationFunctionType

B, N, D, H, DH = 8, 512, 1024, 4, 128
EPS = 1e-5
Q_SCALE = DH**-0.5

P = 128
PACK = 4
PASSES = D // (P * PACK)
TILES = N // P
ROW_TILES = B * TILES
PAIR = 2
HEADS = H + 1
HALF = DH // 2
BN_MAX = 512
W_COLS = H * DH + 2 * DH

QUANT_TILES = 2
MX_LEAD = 1
G_LEAD = QUANT_TILES
T_LEAD = G_LEAD + 1
Y_LEAD = G_LEAD + 2
STAT_LEAD = Y_LEAD + 1
SUM_LEAD = Y_LEAD + 2
FOLD_LEAD = SUM_LEAD + 1
VECTOR_STAT_TILES = 2
LAST_FOLDED = ROW_TILES - 3
FOLDS = D // P

FLOPS = 2 * B * N * D * W_COLS


def tile_attention_pa_t_kernel(tc, x, gamma, wq, wk, wv, sin, cos, out_0, out_1, out_2):
    nc = tc.nc
    with ExitStack() as ctx:
        const = ctx.enter_context(tc.tile_pool(name="const", bufs=1))
        x_pool = ctx.enter_context(tc.tile_pool(name="x_pool", bufs=B))
        stat_pool = ctx.enter_context(tc.tile_pool(name="stat_pool", bufs=6))
        unread_pool = ctx.enter_context(tc.tile_pool(name="unread_pool", bufs=2))
        y_pool = ctx.enter_context(tc.tile_pool(name="y_pool", bufs=4))
        mx_pool = ctx.enter_context(tc.tile_pool(name="mx_pool", bufs=2))
        out_pool = ctx.enter_context(tc.tile_pool(name="out_pool", bufs=4))
        xt_psum = ctx.enter_context(tc.psum_pool(name="xt_psum", bufs=3))
        fold_psum = ctx.enter_context(tc.psum_pool(name="fold_psum", bufs=1))
        q_psum = ctx.enter_context(tc.psum_pool(name="q_psum", bufs=2))
        kv_psum = ctx.enter_context(tc.psum_pool(name="kv_psum", bufs=2))

        ident = const.tile([P, P], FP32)
        make_identity(nc, ident[:])
        ident_bf = const.tile([P, P], BF16)
        make_identity(nc, ident_bf[:])

        ctx.enter_context(tc.manual_schedule())

        x_sb = [x_pool.tile([P, TILES, D], BF16, name="x_sb") for b in range(B)]

        def load_x(b, tiles):
            nc.sync.dma_start(out=x_sb[b][:, tiles, :], in_=x[b].rearrange("(p t) k -> p t k", t=TILES)[:, tiles, :])

        wq_raw = const.tile([P, PASSES, PACK, H * DH], BF16)
        wk_raw = const.tile([P, PASSES, PACK, DH], BF16)
        wv_raw = const.tile([P, PASSES, PACK, DH], BF16)
        gamma_bf = const.tile([P, PASSES, PACK], BF16)
        cos_bf = const.tile([P, TILES, DH], BF16)
        sin_bf = const.tile([P, TILES, DH], BF16)

        load_x(0, slice(0, 1))
        nc.sync.dma_start(out=wk_raw[:], in_=wk.rearrange("(g p j) n -> p g j n", g=PASSES, j=PACK))
        nc.sync.dma_start(out=wv_raw[:], in_=wv.rearrange("(g p j) n -> p g j n", g=PASSES, j=PACK))
        load_x(0, slice(1, 2))
        nc.sync.dma_start(out=gamma_bf[:], in_=gamma.rearrange("(g p j) -> p g j", g=PASSES, j=PACK))
        for g in range(PASSES):
            k_rows = slice(g * P * PACK, (g + 1) * P * PACK)
            nc.sync.dma_start(out=wq_raw[:, g, :, :], in_=wq[k_rows, :].rearrange("(p j) n -> p j n", j=PACK))
        load_x(0, slice(2, 3))
        nc.sync.dma_start(out=cos_bf[:], in_=cos.rearrange("(p t) d -> p t d", t=TILES))
        nc.sync.dma_start(out=sin_bf[:], in_=sin.rearrange("(p t) d -> p t d", t=TILES))
        load_x(0, slice(3, 4))
        for b in range(1, B):
            load_x(b, slice(0, TILES))

        one = const.tile([P, 1], FP32)
        nc.vector.memset(one[:], 1.0)
        root_of_one = const.tile([P, 1], FP32)
        nc.scalar.activation(out=root_of_one[:], in_=one[:], func=ACT.Abs_reciprocal_sqrt)

        sign = const.tile([P, HALF, 2], FP32)
        nc.gpsimd.memset(sign[:, :, 0], -1.0)
        nc.gpsimd.memset(sign[:, :, 1], 1.0)
        cos_q = const.tile([P, TILES, DH], FP32)
        sin_q = const.tile([P, TILES, DH], FP32)
        sin_k = const.tile([P, TILES, DH], FP32)
        gamma_col = const.tile([P, PASSES, PACK], FP32)

        def prepare_tables():
            nc.gpsimd.tensor_scalar(out=cos_q[:], in0=cos_bf[:], scalar1=Q_SCALE, scalar2=0.0, op0=ALU.mult, op1=ALU.add)
            signs = sign[:].rearrange("p i m -> p (i m)").unsqueeze(1).to_broadcast([P, TILES, DH])
            nc.gpsimd.tensor_tensor(out=sin_k[:], in0=sin_bf[:], in1=signs, op=ALU.mult)
            nc.gpsimd.tensor_scalar(out=sin_q[:], in0=sin_k[:], scalar1=Q_SCALE, scalar2=0.0, op0=ALU.mult, op1=ALU.add)

        w_grouped = {}
        w_codes = {}
        w_scales = {}
        for part, width in (("q", H * DH), ("kv", 2 * DH)):
            w_grouped[part] = const.tile([P, PASSES, width, PACK], BF16, name="w_grouped_" + part, align_bytes=64)
            w_codes[part] = const.tile([P, PASSES, width], U32, name="w_codes_" + part, align_bytes=64)
            w_scales[part] = const.tile([P, PASSES, width], U8, name="w_scales_" + part, align_bytes=64)

        def group_wq(g):
            nc.vector.tensor_copy(out=w_grouped["q"][:, g, :, :], in_=wq_raw[:, g, :, :].rearrange("p j n -> p n j"))

        def group_wk_or_wv(raw, cols):
            for g in range(PASSES):
                nc.gpsimd.tensor_scalar(
                    out=w_grouped["kv"][:, g, cols, :],
                    in0=raw[:, g, :, :].rearrange("p j n -> p n j"),
                    scalar1=1.0,
                    scalar2=0.0,
                    op0=ALU.mult,
                    op1=ALU.add,
                )

        def quantise_weights(part):
            nc.vector.quantize_mx(
                out=w_codes[part][:].rearrange("p g n -> p (g n)").bitcast(FP8X4),
                scales=w_scales[part][:].rearrange("p g n -> p (g n)"),
                in_=w_grouped[part][:].rearrange("p g n j -> p (g n j)"),
            )

        neg_mean = {}
        spread = {}
        minus = {}
        rstd = {}
        shift = {}
        y = {}
        xt = {}
        grouped = {}
        codes = {}
        scales = {}
        q_ps = {}
        kv_ps = {}
        rotated = {}
        sin_part = {}
        v_sb = {}

        def on_scalar(i):
            return i < TILES or i % 2 == 1

        def vector_statistics(i):
            b, t = divmod(i, TILES)
            parts = stat_pool.tile([P, D // BN_MAX, 6], FP32, name="parts")
            for h in range(D // BN_MAX):
                nc.vector.bn_stats(out=parts[:, h, :], in_=x_sb[b][:, t, h * BN_MAX : (h + 1) * BN_MAX])
            mean_var = stat_pool.tile([P, 2], FP32, name="mean_var")
            nc.vector.bn_aggr(out=mean_var[:], in_=parts[:].rearrange("p h s -> p (h s)"))
            neg_mean[i] = stat_pool.tile([P, 1], FP32, name="neg_mean")
            nc.vector.tensor_scalar_mul(out=neg_mean[i][:], in0=mean_var[:, 0:1], scalar1=-1.0)
            spread[i] = mean_var[:, 1:2]

        def scalar_sum(values, func, factor, name):
            total = stat_pool.tile([P, 1], FP32, name=name)
            unread = unread_pool.tile([P, D], BF16, name="unread")
            nc.scalar.activation(
                out=unread[:, 0 : values.shape[-1]], in_=values, func=func, scale=factor, accum_out=total[:]
            )
            return total

        def folded(i):
            return VECTOR_STAT_TILES <= i <= LAST_FOLDED and i % 3 != 1

        fold_ps = {}

        def fold(i):
            b, t = divmod(i, TILES)
            fold_ps[i] = fold_psum.tile([P, P], FP32, name="fold_ps")
            for c in range(FOLDS):
                nc.tensor.matmul(
                    fold_ps[i][:],
                    lhsT=ident_bf[:],
                    rhs=x_sb[b][:, t, c * P : (c + 1) * P],
                    start=(c == 0),
                    stop=(c == FOLDS - 1),
                )

        def sum_squares(i):
            if i < VECTOR_STAT_TILES:
                vector_statistics(i)
            else:
                b, t = divmod(i, TILES)
                spread[i] = scalar_sum(x_sb[b][:, t, :], ACT.Square, D**-0.5, "mean_sq")[:]

        def sum_values(i):
            if i >= VECTOR_STAT_TILES:
                b, t = divmod(i, TILES)
                values = fold_ps[i][:] if folded(i) else x_sb[b][:, t, :]
                neg_mean[i] = scalar_sum(values, ACT.Identity, -1.0 / D, "neg_mean")

        def mean_term(i):
            if i >= VECTOR_STAT_TILES:
                minus[i] = stat_pool.tile([P, 1], FP32, name="minus")
                nc.scalar.activation(
                    out=minus[i][:], in_=neg_mean[i][:], func=ACT.Identity, scale=neg_mean[i][:], bias=-EPS
                )

        def inverse_std(i):
            rstd[i] = stat_pool.tile([P, 1], FP32, name="rstd")
            if i < VECTOR_STAT_TILES:
                nc.scalar.activation(out=rstd[i][:], in_=spread[i], func=ACT.Abs_reciprocal_sqrt, bias=EPS)
            else:
                nc.scalar.activation(
                    out=rstd[i][:], in_=spread[i], func=ACT.Abs_reciprocal_sqrt, scale=-1.0, bias=minus[i][:]
                )

        def shift_by_mean(i):
            if on_scalar(i):
                shift[i] = stat_pool.tile([P, 1], FP32, name="shift")
                nc.scalar.activation(out=shift[i][:], in_=rstd[i][:], func=ACT.Identity, scale=neg_mean[i][:])

        def normalise(i):
            b, t = divmod(i, TILES)
            y[i] = y_pool.tile([P, PASSES, PACK, P], FP32, name="y")
            x_rows = x_sb[b][:, t, :].rearrange("p (g m j) -> p g j m", g=PASSES, j=PACK)
            if on_scalar(i):
                nc.scalar.activation(out=y[i][:], in_=x_rows, func=ACT.Identity, scale=rstd[i][:], bias=shift[i][:])
            else:
                nc.gpsimd.tensor_scalar(
                    out=y[i][:], in0=x_rows, scalar1=neg_mean[i][:], scalar2=rstd[i][:], op0=ALU.add, op1=ALU.mult
                )

        def transpose(i):
            xt[i] = [xt_psum.tile([P, PACK, P], FP32, name="xt") for g in range(PASSES)]
            for g in range(PASSES):
                for j in range(PACK):
                    nc.tensor.transpose(xt[i][g][:, j, :], y[i][:, g, j, :], ident[:])

        def scale_by_gamma(i):
            group, slot = divmod(i, QUANT_TILES)
            if slot == 0:
                grouped[group] = mx_pool.tile([P, QUANT_TILES, PASSES, P, PACK], BF16, name="grouped", align_bytes=64)
            for g in range(PASSES):
                nc.vector.tensor_tensor(
                    out=grouped[group][:, slot, g, :, :],
                    in0=xt[i][g][:].rearrange("p j r -> p r j"),
                    in1=gamma_col[:, g, :].unsqueeze(1).to_broadcast([P, P, PACK]),
                    op=ALU.mult,
                )

        def quantise(group):
            codes[group] = mx_pool.tile([P, QUANT_TILES, PASSES, P], U32, name="codes", align_bytes=64)
            scales[group] = mx_pool.tile([P, QUANT_TILES, PASSES, P], U8, name="scales", align_bytes=64)
            nc.vector.quantize_mx(
                out=codes[group][:].rearrange("p s g r -> p (s g r)").bitcast(FP8X4),
                scales=scales[group][:].rearrange("p s g r -> p (s g r)"),
                in_=grouped[group][:].rearrange("p s g r j -> p (s g r j)"),
            )

        def project(i):
            group, slot = divmod(i, QUANT_TILES)
            pair, half = divmod(i, PAIR)
            q_ps[i] = q_psum.tile([P, H * DH], FP32, name="q_ps")
            if half == 0:
                kv_ps[pair] = kv_psum.tile([P, PAIR, 2 * DH], FP32, name="kv_ps")
            for acc, part in ((q_ps[i][:], "q"), (kv_ps[pair][:, half, :], "kv")):
                for g in range(PASSES):
                    nc.tensor.matmul_mx(
                        out=acc,
                        lhsT=codes[group][:, slot, g, :].bitcast(FP8X4),
                        lhsT_scale=scales[group][:, slot, g, :],
                        rhs=w_codes[part][:, g, :].bitcast(FP8X4),
                        rhs_scale=w_scales[part][:, g, :],
                        start=(g == 0),
                        stop=(g == PASSES - 1),
                    )

        def rotary_products(u, cos_table, sin_table, cos_out, sin_out):
            nc.vector.tensor_tensor(out=cos_out, in0=u, in1=cos_table, op=ALU.mult)
            swapped = u.rearrange("p a (i m) -> p a i m", m=2)[:, :, :, ::-1]
            nc.vector.tensor_tensor(
                out=sin_out.rearrange("p a (i m) -> p a i m", m=2),
                in0=swapped,
                in1=sin_table.rearrange("p a (i m) -> p a i m", m=2),
                op=ALU.mult,
            )

        def rotate_q(i):
            pair, half = divmod(i, PAIR)
            t = i % TILES
            if half == 0:
                rotated[pair] = out_pool.tile([P, HEADS, PAIR, DH], FP32, name="rotated")
                sin_part[pair] = out_pool.tile([P, HEADS, PAIR, DH], FP32, name="sin_part")
            rotary_products(
                u=q_ps[i][:].rearrange("p (h d) -> p h d", h=H),
                cos_table=cos_q[:, t, :].unsqueeze(1).to_broadcast([P, H, DH]),
                sin_table=sin_q[:, t, :].unsqueeze(1).to_broadcast([P, H, DH]),
                cos_out=rotated[pair][:, 0:H, half, :],
                sin_out=sin_part[pair][:, 0:H, half, :],
            )

        def tiles_of_pair(pair):
            b, t = divmod(pair * PAIR, TILES)
            return b, slice(t, t + PAIR)

        def copy_v(pair):
            v_sb[pair] = out_pool.tile([P, PAIR, DH], FP32, name="v_sb")
            nc.scalar.copy(out=v_sb[pair][:], in_=kv_ps[pair][:, :, DH : 2 * DH])

        def rotate_k(pair):
            b, ts = tiles_of_pair(pair)
            rotary_products(
                u=kv_ps[pair][:, :, 0:DH],
                cos_table=cos_bf[:, ts, :],
                sin_table=sin_k[:, ts, :],
                cos_out=rotated[pair][:, H, :, :],
                sin_out=sin_part[pair][:, H, :, :],
            )

        def rotary_sum(engine, pair, heads, halves):
            engine.tensor_tensor(
                out=rotated[pair][:, heads, halves, :],
                in0=rotated[pair][:, heads, halves, :],
                in1=sin_part[pair][:, heads, halves, :],
                op=ALU.add,
            )

        def sum_q(i):
            pair, half = divmod(i, PAIR)
            rotary_sum(nc.gpsimd if i < ROW_TILES - 1 else nc.vector, pair, slice(0, H), half)

        def sum_k(pair):
            rotary_sum(nc.gpsimd, pair, H, slice(0, PAIR))

        def store(pair):
            b, ts = tiles_of_pair(pair)
            nc.sync.dma_start(
                out=out_0[b].rearrange("h (p t) d -> p h t d", t=TILES)[:, :, ts, :], in_=rotated[pair][:, 0:H, :, :]
            )
            nc.sync.dma_start(out=out_1[b].rearrange("(p t) d -> p t d", t=TILES)[:, ts, :], in_=rotated[pair][:, H, :, :])
            nc.sync.dma_start(out=out_2[b].rearrange("(p t) d -> p t d", t=TILES)[:, ts, :], in_=v_sb[pair][:])

        def is_tile(i):
            return 0 <= i < ROW_TILES

        def ends(i, size):
            return is_tile(i) and i % size == size - 1

        for s in range(-SUM_LEAD, ROW_TILES + 1):
            y_tile, stat_tile, sum_tile, fold_tile = s + Y_LEAD, s + STAT_LEAD, s + SUM_LEAD, s + FOLD_LEAD
            if sum_tile == 1:
                group_wk_or_wv(wk_raw, slice(0, DH))
            if sum_tile == 3:
                prepare_tables()
                group_wk_or_wv(wv_raw, slice(DH, 2 * DH))
            if 0 <= stat_tile < VECTOR_STAT_TILES:
                inverse_std(stat_tile)
                shift_by_mean(stat_tile)
                normalise(stat_tile)
            if stat_tile == 0:
                transpose(stat_tile)
            if is_tile(y_tile) and not on_scalar(y_tile):
                normalise(y_tile)
            if is_tile(stat_tile):
                mean_term(stat_tile)
            if ends(s - 1, PAIR):
                copy_v((s - 1) // PAIR)
            if is_tile(sum_tile):
                sum_squares(sum_tile)
            if is_tile(stat_tile) and stat_tile >= VECTOR_STAT_TILES:
                inverse_std(stat_tile)
            if is_tile(sum_tile):
                sum_values(sum_tile)
            if is_tile(y_tile) and on_scalar(y_tile) and y_tile >= VECTOR_STAT_TILES:
                normalise(y_tile)
            if is_tile(stat_tile) and stat_tile >= VECTOR_STAT_TILES:
                shift_by_mean(stat_tile)
            if sum_tile == VECTOR_STAT_TILES:
                nc.vector.tensor_copy(out=gamma_col[:], in_=gamma_bf[:])
                group_wq(0)
                group_wq(1)
            if is_tile(s + G_LEAD):
                scale_by_gamma(s + G_LEAD)
            if s + G_LEAD == 1:
                quantise_weights("q")
                quantise_weights("kv")
            if is_tile(s + T_LEAD) and s + T_LEAD > 0:
                transpose(s + T_LEAD)
            if s == ROW_TILES - 1:
                rotate_k(s // PAIR)
                sum_k(s // PAIR)
            if is_tile(s):
                rotate_q(s)
                sum_q(s)
            if ends(s + G_LEAD, QUANT_TILES):
                quantise((s + G_LEAD) // QUANT_TILES)
            if is_tile(s + MX_LEAD):
                project(s + MX_LEAD)
            if is_tile(fold_tile) and folded(fold_tile):
                fold(fold_tile)
            if ends(s, PAIR) and s < ROW_TILES - 1:
                rotate_k(s // PAIR)
                sum_k(s // PAIR)
            if ends(s - 1, PAIR):
                store((s - 1) // PAIR)
